import numpy as np
import ml_dtypes


def mxq(x, axis, fmt="e4m3"):
    dtype, down = {"e4m3": (ml_dtypes.float8_e4m3fn, 7), "e5m2": (ml_dtypes.float8_e5m2, 14)}[fmt]
    v = np.moveaxis(np.asarray(x, np.float32).astype(ml_dtypes.bfloat16).astype(np.float64), axis, -1)
    blocks = v.reshape(v.shape[:-1] + (-1, 32))
    amax = np.abs(blocks).max(-1, keepdims=True)
    byte = np.maximum(np.where(amax > 0, np.frexp(amax)[1] - 1 + 127, 0) - down, 1)
    scale = np.exp2(byte - 127.0)
    codes = (blocks / scale).astype(np.float32).astype(dtype).astype(np.float64)
    return np.moveaxis((codes * scale).reshape(v.shape), -1, axis)


WIDE = False


def mx_kscale(k):
    if not WIDE:
        return np.ones(k)
    levels = np.array([10, -10, 5, -5, 0])
    if k % 512:
        return np.exp2(np.random.permutation(np.resize(levels, k // 32))).repeat(32)
    a = np.empty((k // 512, 16))
    for p in range(k // 512):
        a[p, :8] = np.random.permutation(np.resize(levels, 8))
        for g in range(8):
            far = levels[np.abs(levels - a[p, g]) >= 10]
            a[p, g + 8] = far[np.random.randint(len(far))]
    return np.exp2(a.ravel()).repeat(32)


BF16 = ml_dtypes.bfloat16


def bf(x):
    return np.asarray(x, np.float32).astype(BF16)


def f64(x):
    return np.asarray(x).astype(np.float64)


B, S, D, H, KV, DH, QB = 4, 2048, 512, 2, 1, 128, 512
HALF = DH // 2
EPS = 1e-6


def rope_tables():
    inv_freq = 1.0 / (10000.0 ** (np.arange(HALF) / HALF))
    ang = np.arange(S)[:, None] * inv_freq[None, :]
    ang = np.concatenate([ang, ang], axis=-1)
    return np.sin(ang), np.cos(ang)


def rmsnorm(u, scale, shift):
    rms = np.sqrt(np.mean(u * u, axis=-1, keepdims=True) + EPS)
    return u / rms * (1.0 + scale) + shift


def apply_rope(u, sin, cos):
    rot = np.concatenate([-u[..., HALF:], u[..., :HALF]], axis=-1)
    return u * cos[None, None, :S, :] + rot * sin[None, None, :S, :]


def heads(u, n):
    return u.reshape(B, S, n, DH).transpose(0, 2, 1, 3)


def setup_inputs():
    s = mx_kscale(D)
    sin, cos = rope_tables()
    return {"x": bf(np.random.standard_normal((B, S, D)) * s),
            "sin_thetas": bf(sin), "cos_thetas": bf(cos),
            "wq": bf(np.random.standard_normal((H * DH, D)) / np.sqrt(D) / s),
            "wk": bf(np.random.standard_normal((KV * DH, D)) / np.sqrt(D) / s),
            "wv": bf(np.random.standard_normal((KV * DH, D)) * 2.0 / np.sqrt(D) / s),
            "q_scale": bf(np.random.standard_normal(DH) * 0.1), "q_shift": bf(np.random.standard_normal(DH) * 0.1),
            "k_scale": bf(np.random.standard_normal(DH) * 0.1), "k_shift": bf(np.random.standard_normal(DH) * 0.1)}


def reference(x, sin_thetas, cos_thetas, wq, wk, wv, q_scale, q_shift, k_scale, k_shift):
    xq = mxq(f64(x), 2, "e4m3")
    q = heads(xq @ mxq(f64(wq), 1, "e4m3").T, H)
    k = heads(xq @ mxq(f64(wk), 1, "e4m3").T, KV)
    v = heads(xq @ mxq(f64(wv), 1, "e4m3").T, KV)
    q = rmsnorm(q, f64(q_scale), f64(q_shift))
    k = rmsnorm(k, f64(k_scale), f64(k_shift))
    q = apply_rope(q, f64(sin_thetas), f64(cos_thetas))
    k = apply_rope(k, f64(sin_thetas), f64(cos_thetas))
    return q, k, v

@@ -1,0 +1,446 @@
+from contextlib import ExitStack
+
+import concourse.mybir as mybir
+from concourse.masks import make_identity
+
+F32 = mybir.dt.float32
+BF16 = mybir.dt.bfloat16
+U32 = mybir.dt.uint32
+U8 = mybir.dt.uint8
+FP8X4 = mybir.dt.float8_e4m3fn_x4
+ALU = mybir.AluOpType
+ACT = mybir.ActivationFunctionType
+
+B, S, D = 4, 2048, 512
+P = 128
+DH = 128
+HALF = DH // 2
+NT = 4
+GROUP = P * NT
+PG = S // GROUP
+NH = 3
+EPS = 1e-6
+FLOPS = 2 * B * S * D * 512
+
+
+def tile_groupqueryattention_pa_t_kernel(
+    tc, x, sin_thetas, cos_thetas, wq, wk, wv, q_scale, q_shift, k_scale, k_shift, out_0, out_1, out_2
+):
+    nc = tc.nc
+    with ExitStack() as ctx:
+        const = ctx.enter_context(tc.tile_pool(name="const", bufs=1))
+        xpool = ctx.enter_context(tc.tile_pool(name="xpool", bufs=1))
+        tabs = ctx.enter_context(tc.tile_pool(name="tabs", bufs=1))
+        work = ctx.enter_context(tc.tile_pool(name="work", bufs=2))
+        deep = ctx.enter_context(tc.tile_pool(name="deep", bufs=3))
+        single = ctx.enter_context(tc.tile_pool(name="single", bufs=1))
+        psum_t = ctx.enter_context(tc.psum_pool(name="psum_t", bufs=2))
+        psum_u = ctx.enter_context(tc.psum_pool(name="psum_u", bufs=4))
+        psum_c = ctx.enter_context(tc.psum_pool(name="psum_c", bufs=2))
+        ctx.enter_context(tc.manual_schedule())
+
+        order = [(pg, b) for pg in range(PG) for b in range(B)]
+
+        ident_f = const.tile([P, P], F32, name="ident_f")
+        make_identity(nc, ident_f[:])
+
+        def load_x(gi):
+            pg, b = order[gi]
+            xs = xpool.tile([P, NT, D], BF16, name="xs%d" % gi)
+            nc.sync.dma_start(
+                out=xs[:].rearrange("p n k -> p (n k)"),
+                in_=x[b, pg * GROUP:(pg + 1) * GROUP, :].rearrange("(p n) k -> p (n k)", n=NT),
+            )
+            x_sb.append(xs)
+
+        def load_cs(eng, pg):
+            for c, tab in enumerate((cos_thetas, sin_thetas)):
+                eng.dma_start(
+                    out=cs_sb[:, c, pg * NT:(pg + 1) * NT, :],
+                    in_=tab[pg * GROUP:(pg + 1) * GROUP, :].rearrange("(p n) j -> p n j", n=NT),
+                )
+
+        x_sb = []
+        w_sb = const.tile([P, NT, D], BF16, name="w_sb")
+        vrow = const.tile([P, 4, DH], BF16, name="vrow")
+        nc.vector.memset(vrow[:], 0.0)
+        ones_b = const.tile([P, P], BF16, name="ones_b")
+        nc.vector.memset(ones_b[:], 1.0)
+        vectors = (q_scale, k_scale, q_shift, k_shift)
+
+        def load_vector(i):
+            nc.scalar.dma_start(out=vrow[0:1, i, :], in_=vectors[i].rearrange("(o j) -> o j", o=1))
+
+        def spread_vectors(i0):
+            spread = psum_t.tile([P, 2, DH], F32, tag="xt", name="spread")
+            nc.tensor.matmul(
+                spread[:].rearrange("p i j -> p (i j)"), lhsT=ones_b[:],
+                rhs=vrow[:, i0:i0 + 2, :].rearrange("p i j -> p (i j)"), start=True, stop=True,
+            )
+            return spread
+
+        cs_sb = const.tile([P, 2, PG * NT, DH], BF16, name="cs_sb")
+        nc.sync.dma_start(out=w_sb[:, 0:2, :], in_=wq.rearrange("(r p) k -> p r k", p=P))
+        nc.sync.dma_start(out=w_sb[:, 2, :], in_=wk)
+        nc.sync.dma_start(out=w_sb[:, 3, :], in_=wv)
+        load_x(0)
+        load_vector(0)
+        load_vector(1)
+        load_cs(nc.scalar, 0)
+        load_vector(2)
+        load_vector(3)
+        load_x(1)
+        load_cs(nc.sync, 1)
+        load_x(2)
+        load_x(3)
+        load_cs(nc.sync, 2)
+        load_x(4)
+        load_x(5)
+        load_cs(nc.sync, 3)
+        for gi in range(6, len(order)):
+            load_x(gi)
+
+        eps_t = const.tile([P, 1], F32, name="eps_t")
+        nc.vector.memset(eps_t[:], EPS)
+        warm = const.tile([P, 1], F32, name="warm")
+        nc.scalar.activation(out=warm[:], in_=eps_t[:], func=ACT.Abs_reciprocal_sqrt)
+
+        ident_b = const.tile([P, P], BF16, name="ident_b")
+        nc.vector.tensor_copy(out=ident_b[:], in_=ident_f[:])
+        perm_f = const.tile([P, P], F32, name="perm_f")
+        nc.vector.tensor_copy(out=perm_f[:, 0:HALF], in_=ident_f[:, HALF:])
+        nc.vector.tensor_copy(out=perm_f[:, HALF:], in_=ident_f[:, 0:HALF])
+
+        g3 = const.tile([P, NH, DH], F32, name="g3")
+        scales_ps = spread_vectors(0)
+        nc.vector.tensor_scalar_add(out=g3[:, 0:2, :], in0=scales_ps[:, 0:1, :].to_broadcast([P, 2, DH]), scalar1=1.0)
+        nc.vector.tensor_scalar_add(out=g3[:, 2, :], in0=scales_ps[:, 1, :], scalar1=1.0)
+        gs3 = const.tile([P, NH, DH], F32, name="gs3")
+        nc.vector.tensor_copy(out=gs3[:, :, 0:HALF], in_=g3[:, :, 0:HALF])
+        nc.vector.tensor_scalar_mul(out=gs3[:, :, HALF:], in0=g3[:, :, HALF:], scalar1=-1.0)
+
+        dc = const.tile([P, 2, DH], BF16, name="dc")
+        ds = const.tile([P, 2, DH], BF16, name="ds")
+        dg = const.tile([P, 2, 2, DH], F32, name="dg")
+        bsrc = const.tile([P, 4, DH], F32, name="bsrc")
+        colv = const.tile([P, 4], F32, name="colv")
+
+        nc.vector.tensor_copy(out=bsrc[:, 0:2, :], in_=g3[:, 1:3, :])
+        nc.vector.tensor_copy(out=bsrc[:, 2:4, 0:HALF], in_=gs3[:, 1:3, HALF:])
+        nc.vector.tensor_copy(out=bsrc[:, 2:4, HALF:], in_=gs3[:, 1:3, 0:HALF])
+
+        def small_tables():
+            shifts_ps = spread_vectors(2)
+            nc.vector.tensor_tensor(
+                out=dc[:], in0=shifts_ps[:], in1=ident_b[:].unsqueeze(1).to_broadcast([P, 2, DH]), op=ALU.mult
+            )
+            nc.vector.scalar_tensor_tensor(
+                out=ds[:, :, 0:HALF], in0=shifts_ps[:, :, HALF:], scalar=-1.0,
+                in1=ident_b[:, 0:HALF].unsqueeze(1).to_broadcast([P, 2, HALF]), op0=ALU.mult, op1=ALU.mult,
+            )
+            nc.vector.tensor_tensor(
+                out=ds[:, :, HALF:], in0=shifts_ps[:, :, 0:HALF],
+                in1=ident_b[:, HALF:].unsqueeze(1).to_broadcast([P, 2, HALF]), op=ALU.mult,
+            )
+            col_ps = psum_t.tile([P, 4, P], F32, tag="xt", name="col_ps")
+            for i in range(4):
+                nc.tensor.transpose(col_ps[:, i, :], bsrc[:, i, :], ident_f[:])
+            nc.scalar.copy(out=colv[:], in_=col_ps[:, :, 0])
+            for i in range(4):
+                nc.scalar.activation(
+                    out=dg[:, i // 2, i % 2, :], in_=ident_f[:] if i < 2 else perm_f[:], func=ACT.Copy,
+                    scale=colv[:, i:i + 1],
+                )
+
+        NG = len(order)
+        w_codes = const.tile([P, NT * P], U32, name="w_codes", align_bytes=64)
+        w_scales = const.tile([P, NT * P], U8, name="w_scales", align_bytes=64)
+        state = {}
+        g12_tiles = {}
+        cst_tiles = {}
+        c_tiles = {}
+        cq_tiles = {}
+
+        def transpose_group(src, share=False):
+            grouped = work.tile([P, NT, P, 4], BF16, tag="grouped", name="grouped", align_bytes=64)
+            gwords = grouped[:].bitcast(F32)
+            banks = []
+            for half in range(2):
+                xt = psum_t.tile([P, 2, 2, P], F32, tag="xt", name="xt")
+                for i in range(2):
+                    words = src[:, 2 * half + i, :].bitcast(F32)
+                    for u in range(2):
+                        nc.tensor.transpose(xt[:, i, u, :], words[:, u:2 * P:2], ident_f[:])
+                banks.append(xt)
+            for half in range(2):
+                dst = gwords[:, 2 * half:2 * half + 2, :, :]
+                if share and half == 1:
+                    nc.vector.tensor_copy(out=dst, in_=banks[half][:].rearrange("p i u r -> p i r u"))
+                else:
+                    nc.scalar.copy(out=dst, in_=banks[half][:].rearrange("p i u r -> p i r u"))
+            return grouped
+
+        def quantise(grouped, codes, scales):
+            nc.vector.quantize_mx(
+                out=codes[:].bitcast(FP8X4), scales=scales[:], in_=grouped[:].rearrange("p n r t -> p (n r t)")
+            )
+
+        def table_g1(eng, pg, n0, n1):
+            g12 = g12_tiles[pg]
+            k = n1 - n0
+            cosv = cs_sb[:, 0, pg * NT + n0:pg * NT + n1, :]
+            eng.tensor_tensor(
+                out=g12[:, n0:n1, 0, :, :], in0=cosv.unsqueeze(2).to_broadcast([P, k, NH, DH]),
+                in1=g3[:].unsqueeze(1).to_broadcast([P, k, NH, DH]), op=ALU.mult,
+            )
+
+        def table_g2(eng, pg, n0, n1, c):
+            g12 = g12_tiles[pg]
+            k = n1 - n0
+            sinv = cs_sb[:, 1, pg * NT + n0:pg * NT + n1, (1 - c) * HALF:(2 - c) * HALF]
+            eng.tensor_tensor(
+                out=g12[:, n0:n1, 1, :, c * HALF:(c + 1) * HALF],
+                in0=sinv.unsqueeze(2).to_broadcast([P, k, NH, HALF]),
+                in1=gs3[:, :, c * HALF:(c + 1) * HALF].unsqueeze(1).to_broadcast([P, k, NH, HALF]), op=ALU.mult,
+            )
+
+        def table_t(pg):
+            cst_ps = psum_t.tile([P, 2, NT, P], BF16, tag="xt", name="cst_ps")
+            for c in range(2):
+                for n in range(NT):
+                    nc.tensor.transpose(cst_ps[:, c, n, :], cs_sb[:, c, pg * NT + n, :], ident_b[:])
+            cst = work.tile([P, 2, NT, P], BF16, tag="cst", name="cst")
+            nc.scalar.copy(out=cst[:], in_=cst_ps[:])
+            cst_tiles[pg] = cst
+
+        def table_c(pg):
+            cst = cst_tiles[pg]
+            pair = []
+            for half in range(2):
+                c_ps = psum_c.tile([P, 2, 2, DH], F32, tag="c", name="c_ps")
+                for i in range(2):
+                    n = 2 * half + i
+                    dst = c_ps[:, i, :, :].rearrange("p a j -> p (a j)")
+                    nc.tensor.matmul(
+                        dst, lhsT=cst[:, 0, n, :], rhs=dc[:].rearrange("p a j -> p (a j)"), start=True, stop=False
+                    )
+                    nc.tensor.matmul(
+                        dst, lhsT=cst[:, 1, n, :], rhs=ds[:].rearrange("p a j -> p (a j)"), start=False, stop=True
+                    )
+                pair.append(c_ps)
+            c_tiles[pg] = pair
+            cq_last = const.tile([P, DH], F32, name="cq_last%d" % pg)
+            nc.scalar.copy(out=cq_last[:], in_=pair[1][:, 1, 0, :])
+            cq_tiles[pg] = cq_last
+
+        def front(gi):
+            state[gi] = {"grouped": transpose_group(x_sb[gi], share=(gi < 2))}
+
+        def table_front(pg, n):
+            if n == 0:
+                cst_tiles[pg] = work.tile([P, 2, NT, P], BF16, tag="cst", name="cst")
+            cs_ps = psum_t.tile([P, 2, P], BF16, tag="xt", name="cs_ps")
+            for c in range(2):
+                nc.tensor.transpose(cs_ps[:, c, :], cs_sb[:, c, pg * NT + n, :], ident_b[:])
+            nc.scalar.copy(out=cst_tiles[pg][:, :, n, :], in_=cs_ps[:])
+            csf = work.tile([P, 2, P], F32, tag="csf", name="csf")
+            nc.scalar.copy(out=csf[:], in_=cs_ps[:])
+            return csf
+
+        def table_back(pg, n, csf):
+            gt = psum_t.tile([P, 2, 2, P], F32, tag="xt", name="gt")
+            for a in range(2):
+                nc.tensor.matmul(
+                    gt[:, a, :, :].rearrange("p q j -> p (q j)"), lhsT=csf[:, a, :],
+                    rhs=dg[:, a, :, :].rearrange("p q j -> p (q j)"), start=True, stop=True,
+                )
+            g12 = g12_tiles[pg]
+            nc.scalar.copy(out=g12[:, n, :, 0:2, :], in_=gt[:, :, 0:1, :].to_broadcast([P, 2, 2, DH]))
+            nc.scalar.copy(out=g12[:, n, :, 2, :], in_=gt[:, :, 1, :])
+
+        def quant(gi):
+            st = state[gi]
+            st["codes"] = deep.tile([P, NT * P], U32, tag="codes", name="codes", align_bytes=64)
+            st["scales"] = deep.tile([P, NT * P], U8, tag="scales", name="scales", align_bytes=64)
+            quantise(st["grouped"], st["codes"], st["scales"])
+
+        def project(gi, n):
+            st = state[gi]
+            if n == 0:
+                st["ss"] = deep.tile([P, NT * NH], F32, tag="ss", name="ss")
+                st["ov"] = deep.tile([P, NT, DH], F32, tag="ov", name="ov")
+                st["u"] = []
+            codes, scales, ss, ov = st["codes"], st["scales"], st["ss"], st["ov"]
+            u = psum_u.tile([P, 4 * DH], F32, tag="u", name="u")
+            st["u"].append(u)
+            nc.tensor.matmul_mx(
+                out=u[:],
+                lhsT=codes[:, n * P:(n + 1) * P].bitcast(FP8X4),
+                lhsT_scale=scales[:, n * P:(n + 1) * P],
+                rhs=w_codes[:].bitcast(FP8X4),
+                rhs_scale=w_scales[:],
+                start=True,
+                stop=True,
+            )
+            for h in range(NH):
+                junk = work.tile([P, DH], BF16, tag="junk", name="junk")
+                nc.scalar.activation(
+                    out=junk[:], in_=u[:, h * DH:(h + 1) * DH], func=ACT.Square,
+                    accum_out=ss[:, n * NH + h:n * NH + h + 1],
+                )
+            nc.scalar.copy(out=ov[:, n, :], in_=u[:, NH * DH:])
+
+        def norm_root(gi):
+            pg, b = order[gi]
+            st = state[gi]
+            st["rinv"] = deep.tile([P, NT * NH], F32, tag="rinv", name="rinv")
+            nc.scalar.activation(
+                out=st["rinv"][:], in_=st["ss"][:], func=ACT.Abs_reciprocal_sqrt, scale=1.0 / DH, bias=eps_t[:]
+            )
+            lo = pg * GROUP
+            nc.sync.dma_start(
+                out=out_2[b, 0, lo:lo + GROUP, :].rearrange("(p n) j -> p (n j)", n=NT),
+                in_=st["ov"][:].rearrange("p n j -> p (n j)"),
+            )
+
+        def products(gi, n):
+            pg, b = order[gi]
+            st = state[gi]
+            if n == 0:
+                st["t12"] = deep.tile([P, 2, NT, NH, 2, HALF], F32, tag="t12", name="t12")
+            u = st["u"][n]
+            nc.vector.tensor_tensor(
+                out=st["t12"][:, :, n, :, :, :].rearrange("p a h c j -> p a (h c j)"),
+                in0=u[:, 0:NH * DH].unsqueeze(1).to_broadcast([P, 2, NH * DH]),
+                in1=g12_tiles[pg][:, n, :, :, :].rearrange("p a h j -> p a (h j)"),
+                op=ALU.mult,
+            )
+
+        def join(eng, gi, n0, n1):
+            t12 = state[gi]["t12"]
+            for c in range(2):
+                eng.tensor_tensor(
+                    out=t12[:, 0, n0:n1, :, c, :], in0=t12[:, 0, n0:n1, :, c, :],
+                    in1=t12[:, 1, n0:n1, :, 1 - c, :], op=ALU.add,
+                )
+
+        def join_pool(gi):
+            st = state[gi]
+            t12 = st["t12"]
+            t3 = single.tile([P, NT, NH, 2, HALF], F32, tag="t3", name="t3")
+            st["t3"] = t3
+            for n0 in (0, 2):
+                nc.gpsimd.tensor_tensor(
+                    out=t3[:, n0:n0 + 2, :, :, :].rearrange("p n h c j -> p (n h) c j"),
+                    in0=t12[:, 0, n0:n0 + 2, :, :, :].rearrange("p n h c j -> p (n h) c j"),
+                    in1=t12[:, 1, n0:n0 + 2, :, :, :].rearrange("p n h c j -> p (n h) c j")[:, :, ::-1, :],
+                    op=ALU.add,
+                )
+
+        def finish_pool(gi):
+            pg, b = order[gi]
+            st = state[gi]
+            st["oqk"] = deep.tile([P, NH, NT, DH], F32, tag="oqk", name="oqk")
+            n = NT - 1
+            for h in range(2):
+                nc.gpsimd.tensor_scalar(
+                    out=st["oqk"][:, h, n, :], in0=st["t3"][:, n, h, :, :].rearrange("p c j -> p (c j)"),
+                    scalar1=st["rinv"][:, n * NH + h:n * NH + h + 1], scalar2=0.0, op0=ALU.mult, op1=ALU.add,
+                )
+            nc.gpsimd.tensor_tensor(
+                out=st["oqk"][:, 0:2, n, :], in0=st["oqk"][:, 0:2, n, :],
+                in1=cq_tiles[pg][:].unsqueeze(1).to_broadcast([P, 2, DH]), op=ALU.add,
+            )
+
+        def finish(gi, blocks):
+            pg, b = order[gi]
+            st = state[gi]
+            if "oqk" not in st:
+                st["oqk"] = deep.tile([P, NH, NT, DH], F32, tag="oqk", name="oqk")
+            for n, h in blocks:
+                summed = st["t3"][:, n, h, :, :] if "t3" in st else st["t12"][:, 0, n, h, :, :]
+                nc.vector.scalar_tensor_tensor(
+                    out=st["oqk"][:, h, n, :],
+                    in0=summed.rearrange("p c j -> p (c j)"),
+                    scalar=st["rinv"][:, n * NH + h:n * NH + h + 1],
+                    in1=c_tiles[pg][n // 2][:, n % 2, h // 2, :],
+                    op0=ALU.mult,
+                    op1=ALU.add,
+                )
+
+        def store(gi, n0, n1):
+            pg, b = order[gi]
+            oqk = state[gi]["oqk"]
+            lo = pg * GROUP
+            nc.sync.dma_start(
+                out=out_0[b, :, lo:lo + GROUP, :].rearrange("h (p n) j -> p h n j", n=NT)[:, :, n0:n1, :],
+                in_=oqk[:, 0:2, n0:n1, :],
+            )
+            nc.sync.dma_start(
+                out=out_1[b, 0, lo:lo + GROUP, :].rearrange("(p n) j -> p n j", n=NT)[:, n0:n1, :],
+                in_=oqk[:, 2, n0:n1, :],
+            )
+
+        for pg in range(PG):
+            g12_tiles[pg] = tabs.tile([P, NT, 2, NH, DH], F32, name="g12_%d" % pg)
+
+        def table_tile(eng, pg, n0, n1):
+            table_g1(eng, pg, n0, n1)
+            table_g2(eng, pg, n0, n1, 0)
+            table_g2(eng, pg, n0, n1, 1)
+
+        late_tables = {0: (2, 0), 1: (2, 1), 3: (2, 2), 4: (2, 3), 6: (3, 0), 7: (3, 1), 9: (3, 2), 10: (3, 3)}
+        all_blocks = [(n, h) for n in range(NT) for h in range(NH)]
+        vector_blocks = [blk for blk in all_blocks if blk not in ((NT - 1, 0), (NT - 1, 1))]
+
+        w_grouped = transpose_group(w_sb, share=True)
+        for pg, n in ((0, 0), (0, 1), (1, 0), (1, 1)):
+            table_tile(nc.gpsimd, pg, n, n + 1)
+        quantise(w_grouped, w_codes, w_scales)
+        for it in range(-2, NG + 1):
+            if it + 2 < NG:
+                front(it + 2)
+            if it in late_tables:
+                pg, n = late_tables[it]
+                wide = table_front(pg, n)
+            if 0 <= it - 1 < NG - 1:
+                join_pool(it - 1)
+                if it - 1 >= 2:
+                    finish_pool(it - 1)
+            if it == 1 or it == 2:
+                table_tile(nc.gpsimd, 1, it + 1, it + 2)
+            for n in range(NT):
+                if 0 <= it < NG:
+                    products(it, n)
+                if 0 <= it + 1 < NG:
+                    project(it + 1, n)
+                if it == NG - 1 and n == 1:
+                    join(nc.gpsimd, it, 0, 2)
+            if 0 <= it + 1 < NG:
+                norm_root(it + 1)
+            if it in late_tables:
+                pg, n = late_tables[it]
+                table_back(pg, n, wide)
+            if 0 <= it - 1 < NG - 1:
+                finish(it - 1, (vector_blocks if it - 1 >= 2 else all_blocks)[:-1])
+            if it + 2 < NG:
+                quant(it + 2)
+            if 0 <= it - 1 < NG - 1:
+                finish(it - 1, vector_blocks[-1:])
+                store(it - 1, 0, NT)
+                pg, b = order[it - 1]
+                if b == B - 1 and pg + 1 < PG:
+                    table_c(pg + 1)
+            if it < 0:
+                table_tile(nc.vector, 0, it + NT, it + NT + 1)
+            if it == -1:
+                small_tables()
+                table_t(0)
+                table_c(0)
+            if it == 2:
+                table_t(1)
+            if it - 1 == NG - 1:
+                join(nc.vector, it - 1, 2, NT)
+                for n0 in (2, 0):
+                    finish(it - 1, all_blocks[n0 * NH:(n0 + 2) * NH])
+                    store(it - 1, n0, n0 + 2)

@@ -342,14 +342,14 @@ def tile_groupqueryattention_pa_t_kernel(
             st = state[gi]
             st["oqk"] = deep.tile([P, NH, NT, DH], F32, tag="oqk", name="oqk")
             n = NT - 1
-            for h in range(2):
+            for h in range(1, 2):
                 nc.gpsimd.tensor_scalar(
                     out=st["oqk"][:, h, n, :], in0=st["t3"][:, n, h, :, :].rearrange("p c j -> p (c j)"),
                     scalar1=st["rinv"][:, n * NH + h:n * NH + h + 1], scalar2=0.0, op0=ALU.mult, op1=ALU.add,
                 )
             nc.gpsimd.tensor_tensor(
-                out=st["oqk"][:, 0:2, n, :], in0=st["oqk"][:, 0:2, n, :],
-                in1=cq_tiles[pg][:].unsqueeze(1).to_broadcast([P, 2, DH]), op=ALU.add,
+                out=st["oqk"][:, 1, n, :], in0=st["oqk"][:, 1, n, :],
+                in1=cq_tiles[pg][:], op=ALU.add,
             )
 
         def finish(gi, blocks):
@@ -391,7 +391,7 @@ def tile_groupqueryattention_pa_t_kernel(
 
         late_tables = {0: (2, 0), 1: (2, 1), 3: (2, 2), 4: (2, 3), 6: (3, 0), 7: (3, 1), 9: (3, 2), 10: (3, 3)}
         all_blocks = [(n, h) for n in range(NT) for h in range(NH)]
-        vector_blocks = [blk for blk in all_blocks if blk not in ((NT - 1, 0), (NT - 1, 1))]
+        vector_blocks = [blk for blk in all_blocks if blk not in ((NT - 1, 1),)]
 
         w_grouped = transpose_group(w_sb, share=True)
         for pg, n in ((0, 0), (0, 1), (1, 0), (1, 1)):

@@ -80,17 +80,15 @@ def tile_groupqueryattention_pa_t_kernel(
             return spread
 
         cs_sb = const.tile([P, 2, PG * NT, DH], BF16, name="cs_sb")
+        for i in range(4):
+            load_vector(i)
+        load_cs(nc.sync, 0)
+        load_cs(nc.sync, 1)
         nc.sync.dma_start(out=w_sb[:, 0:2, :], in_=wq.rearrange("(r p) k -> p r k", p=P))
         nc.sync.dma_start(out=w_sb[:, 2, :], in_=wk)
         nc.sync.dma_start(out=w_sb[:, 3, :], in_=wv)
         load_x(0)
-        load_vector(0)
-        load_vector(1)
-        load_cs(nc.scalar, 0)
-        load_vector(2)
-        load_vector(3)
         load_x(1)
-        load_cs(nc.sync, 1)
         load_x(2)
         load_x(3)
         load_cs(nc.sync, 2)
@@ -152,6 +150,8 @@ def tile_groupqueryattention_pa_t_kernel(
                     scale=colv[:, i:i + 1],
                 )
 
+        small_tables()
+
         NG = len(order)
         w_codes = const.tile([P, NT * P], U32, name="w_codes", align_bytes=64)
         w_scales = const.tile([P, NT * P], U8, name="w_scales", align_bytes=64)
@@ -204,8 +204,8 @@ def tile_groupqueryattention_pa_t_kernel(
                 in1=gs3[:, :, c * HALF:(c + 1) * HALF].unsqueeze(1).to_broadcast([P, k, NH, HALF]), op=ALU.mult,
             )
 
-        def table_t(pg):
-            cst_ps = psum_t.tile([P, 2, NT, P], BF16, tag="xt", name="cst_ps")
+        def table_t(pg, pool, tag):
+            cst_ps = pool.tile([P, 2, NT, P], BF16, tag=tag, name="cst_ps")
             for c in range(2):
                 for n in range(NT):
                     nc.tensor.transpose(cst_ps[:, c, n, :], cs_sb[:, c, pg * NT + n, :], ident_b[:])
@@ -234,7 +234,7 @@ def tile_groupqueryattention_pa_t_kernel(
             cq_tiles[pg] = cq_last
 
         def front(gi):
-            state[gi] = {"grouped": transpose_group(x_sb[gi], share=(gi < 2))}
+            state[gi] = {"grouped": transpose_group(x_sb[gi])}
 
         def table_front(pg, n):
             if n == 0:
@@ -393,13 +393,16 @@ def tile_groupqueryattention_pa_t_kernel(
         all_blocks = [(n, h) for n in range(NT) for h in range(NH)]
         vector_blocks = [blk for blk in all_blocks if blk not in ((NT - 1, 1),)]
 
-        w_grouped = transpose_group(w_sb, share=True)
-        for pg, n in ((0, 0), (0, 1), (1, 0), (1, 1)):
-            table_tile(nc.gpsimd, pg, n, n + 1)
+        table_tile(nc.vector, 0, 0, NT)
+        w_grouped = transpose_group(w_sb)
+        for n in range(2):
+            table_tile(nc.gpsimd, 1, n, n + 1)
         quantise(w_grouped, w_codes, w_scales)
         for it in range(-2, NG + 1):
             if it + 2 < NG:
                 front(it + 2)
+            if it == -2:
+                table_t(0, psum_u, "u")
             if it in late_tables:
                 pg, n = late_tables[it]
                 wide = table_front(pg, n)
@@ -412,6 +415,8 @@ def tile_groupqueryattention_pa_t_kernel(
             for n in range(NT):
                 if 0 <= it < NG:
                     products(it, n)
+                if it == 0 and n == 0:
+                    quant(1)
                 if 0 <= it + 1 < NG:
                     project(it + 1, n)
                 if it == NG - 1 and n == 1:
@@ -423,7 +428,7 @@ def tile_groupqueryattention_pa_t_kernel(
                 table_back(pg, n, wide)
             if 0 <= it - 1 < NG - 1:
                 finish(it - 1, (vector_blocks if it - 1 >= 2 else all_blocks)[:-1])
-            if it + 2 < NG:
+            if it + 2 < NG and it != -1:
                 quant(it + 2)
             if 0 <= it - 1 < NG - 1:
                 finish(it - 1, vector_blocks[-1:])
@@ -431,14 +436,10 @@ def tile_groupqueryattention_pa_t_kernel(
                 pg, b = order[it - 1]
                 if b == B - 1 and pg + 1 < PG:
                     table_c(pg + 1)
-            if it < 0:
-                table_tile(nc.vector, 0, it + NT, it + NT + 1)
             if it == -1:
-                small_tables()
-                table_t(0)
                 table_c(0)
             if it == 2:
-                table_t(1)
+                table_t(1, psum_t, "xt")
             if it - 1 == NG - 1:
                 join(nc.vector, it - 1, 2, NT)
                 for n0 in (2, 0):

@@ -159,7 +159,6 @@ def tile_groupqueryattention_pa_t_kernel(
         g12_tiles = {}
         cst_tiles = {}
         c_tiles = {}
-        cq_tiles = {}
 
         def transpose_group(src, share=False):
             grouped = work.tile([P, NT, P, 4], BF16, tag="grouped", name="grouped", align_bytes=64)
@@ -229,9 +228,6 @@ def tile_groupqueryattention_pa_t_kernel(
                     )
                 pair.append(c_ps)
             c_tiles[pg] = pair
-            cq_last = const.tile([P, DH], F32, name="cq_last%d" % pg)
-            nc.scalar.copy(out=cq_last[:], in_=pair[1][:, 1, 0, :])
-            cq_tiles[pg] = cq_last
 
         def front(gi):
             state[gi] = {"grouped": transpose_group(x_sb[gi])}
@@ -337,21 +333,6 @@ def tile_groupqueryattention_pa_t_kernel(
                     op=ALU.add,
                 )
 
-        def finish_pool(gi):
-            pg, b = order[gi]
-            st = state[gi]
-            st["oqk"] = deep.tile([P, NH, NT, DH], F32, tag="oqk", name="oqk")
-            n = NT - 1
-            for h in range(1, 2):
-                nc.gpsimd.tensor_scalar(
-                    out=st["oqk"][:, h, n, :], in0=st["t3"][:, n, h, :, :].rearrange("p c j -> p (c j)"),
-                    scalar1=st["rinv"][:, n * NH + h:n * NH + h + 1], scalar2=0.0, op0=ALU.mult, op1=ALU.add,
-                )
-            nc.gpsimd.tensor_tensor(
-                out=st["oqk"][:, 1, n, :], in0=st["oqk"][:, 1, n, :],
-                in1=cq_tiles[pg][:], op=ALU.add,
-            )
-
         def finish(gi, blocks):
             pg, b = order[gi]
             st = state[gi]
@@ -391,7 +372,7 @@ def tile_groupqueryattention_pa_t_kernel(
 
         late_tables = {0: (2, 0), 1: (2, 1), 3: (2, 2), 4: (2, 3), 6: (3, 0), 7: (3, 1), 9: (3, 2), 10: (3, 3)}
         all_blocks = [(n, h) for n in range(NT) for h in range(NH)]
-        vector_blocks = [blk for blk in all_blocks if blk not in ((NT - 1, 1),)]
+        vector_blocks = all_blocks
 
         table_tile(nc.vector, 0, 0, NT)
         w_grouped = transpose_group(w_sb)
@@ -408,8 +389,6 @@ def tile_groupqueryattention_pa_t_kernel(
                 wide = table_front(pg, n)
             if 0 <= it - 1 < NG - 1:
                 join_pool(it - 1)
-                if it - 1 >= 2:
-                    finish_pool(it - 1)
             if it == 1 or it == 2:
                 table_tile(nc.gpsimd, 1, it + 1, it + 2)
             for n in range(NT):

@@ -370,7 +370,7 @@ def tile_groupqueryattention_pa_t_kernel(
             table_g2(eng, pg, n0, n1, 0)
             table_g2(eng, pg, n0, n1, 1)
 
-        late_tables = {0: (2, 0), 1: (2, 1), 3: (2, 2), 4: (2, 3), 6: (3, 0), 7: (3, 1), 9: (3, 2), 10: (3, 3)}
+        late_tables = {0: (2, 0), 1: (2, 1), 3: (2, 2), 5: (2, 3)}
         all_blocks = [(n, h) for n in range(NT) for h in range(NH)]
         vector_blocks = all_blocks
 
@@ -391,6 +391,13 @@ def tile_groupqueryattention_pa_t_kernel(
                 join_pool(it - 1)
             if it == 1 or it == 2:
                 table_tile(nc.gpsimd, 1, it + 1, it + 2)
+            if 4 <= it < 4 + 2 * NT:
+                n = (it - 4) // 2
+                if it % 2 == 0:
+                    table_g1(nc.gpsimd, 3, n, n + 1)
+                else:
+                    table_g2(nc.gpsimd, 3, n, n + 1, 0)
+                    table_g2(nc.gpsimd, 3, n, n + 1, 1)
             for n in range(NT):
                 if 0 <= it < NG:
                     products(it, n)
@@ -417,8 +424,8 @@ def tile_groupqueryattention_pa_t_kernel(
                     table_c(pg + 1)
             if it == -1:
                 table_c(0)
-            if it == 2:
-                table_t(1, psum_t, "xt")
+            if it == 2 or it == 7:
+                table_t(1 if it == 2 else 3, psum_t, "xt")
             if it - 1 == NG - 1:
                 join(nc.vector, it - 1, 2, NT)
                 for n0 in (2, 0):

@@ -19,6 +19,7 @@ NT = 4
 GROUP = P * NT
 PG = S // GROUP
 NH = 3
+VSHARE = {0: (1,), 1: (1,)}
 EPS = 1e-6
 FLOPS = 2 * B * S * D * 512
 
@@ -68,11 +69,13 @@ def tile_groupqueryattention_pa_t_kernel(
         nc.vector.memset(ones_b[:], 1.0)
         vectors = (q_scale, k_scale, q_shift, k_shift)
 
+        vload = const.tile([1, 4, DH], BF16, name="vload")
+
         def load_vector(i):
-            nc.scalar.dma_start(out=vrow[0:1, i, :], in_=vectors[i].rearrange("(o j) -> o j", o=1))
+            nc.sync.dma_start(out=vload[0:1, i, :], in_=vectors[i].rearrange("(o j) -> o j", o=1))
 
         def spread_vectors(i0):
-            spread = psum_t.tile([P, 2, DH], F32, tag="xt", name="spread")
+            spread = psum_c.tile([P, 2, DH], F32, tag="c", name="spread")
             nc.tensor.matmul(
                 spread[:].rearrange("p i j -> p (i j)"), lhsT=ones_b[:],
                 rhs=vrow[:, i0:i0 + 2, :].rearrange("p i j -> p (i j)"), start=True, stop=True,
@@ -82,6 +85,7 @@ def tile_groupqueryattention_pa_t_kernel(
         cs_sb = const.tile([P, 2, PG * NT, DH], BF16, name="cs_sb")
         for i in range(4):
             load_vector(i)
+        nc.vector.tensor_copy(out=vrow[0:1, :, :], in_=vload[:])
         load_cs(nc.sync, 0)
         load_cs(nc.sync, 1)
         nc.sync.dma_start(out=w_sb[:, 0:2, :], in_=wq.rearrange("(r p) k -> p r k", p=P))
@@ -123,11 +127,10 @@ def tile_groupqueryattention_pa_t_kernel(
         bsrc = const.tile([P, 4, DH], F32, name="bsrc")
         colv = const.tile([P, 4], F32, name="colv")
 
-        nc.vector.tensor_copy(out=bsrc[:, 0:2, :], in_=g3[:, 1:3, :])
-        nc.vector.tensor_copy(out=bsrc[:, 2:4, 0:HALF], in_=gs3[:, 1:3, HALF:])
-        nc.vector.tensor_copy(out=bsrc[:, 2:4, HALF:], in_=gs3[:, 1:3, 0:HALF])
-
         def small_tables():
+            nc.vector.tensor_copy(out=bsrc[:, 0:2, :], in_=g3[:, 1:3, :])
+            nc.vector.tensor_copy(out=bsrc[:, 2:4, 0:HALF], in_=gs3[:, 1:3, HALF:])
+            nc.vector.tensor_copy(out=bsrc[:, 2:4, HALF:], in_=gs3[:, 1:3, 0:HALF])
             shifts_ps = spread_vectors(2)
             nc.vector.tensor_tensor(
                 out=dc[:], in0=shifts_ps[:], in1=ident_b[:].unsqueeze(1).to_broadcast([P, 2, DH]), op=ALU.mult
@@ -140,7 +143,7 @@ def tile_groupqueryattention_pa_t_kernel(
                 out=ds[:, :, HALF:], in0=shifts_ps[:, :, 0:HALF],
                 in1=ident_b[:, HALF:].unsqueeze(1).to_broadcast([P, 2, HALF]), op=ALU.mult,
             )
-            col_ps = psum_t.tile([P, 4, P], F32, tag="xt", name="col_ps")
+            col_ps = psum_c.tile([P, 4, P], F32, tag="c", name="col_ps")
             for i in range(4):
                 nc.tensor.transpose(col_ps[:, i, :], bsrc[:, i, :], ident_f[:])
             nc.scalar.copy(out=colv[:], in_=col_ps[:, :, 0])
@@ -150,8 +153,6 @@ def tile_groupqueryattention_pa_t_kernel(
                     scale=colv[:, i:i + 1],
                 )
 
-        small_tables()
-
         NG = len(order)
         w_codes = const.tile([P, NT * P], U32, name="w_codes", align_bytes=64)
         w_scales = const.tile([P, NT * P], U8, name="w_scales", align_bytes=64)
@@ -160,12 +161,12 @@ def tile_groupqueryattention_pa_t_kernel(
         cst_tiles = {}
         c_tiles = {}
 
-        def transpose_group(src, share=False):
+        def transpose_group(src, share=(), pool=psum_t, tag="xt"):
             grouped = work.tile([P, NT, P, 4], BF16, tag="grouped", name="grouped", align_bytes=64)
             gwords = grouped[:].bitcast(F32)
             banks = []
             for half in range(2):
-                xt = psum_t.tile([P, 2, 2, P], F32, tag="xt", name="xt")
+                xt = pool.tile([P, 2, 2, P], F32, tag=tag, name="xt")
                 for i in range(2):
                     words = src[:, 2 * half + i, :].bitcast(F32)
                     for u in range(2):
@@ -173,7 +174,7 @@ def tile_groupqueryattention_pa_t_kernel(
                 banks.append(xt)
             for half in range(2):
                 dst = gwords[:, 2 * half:2 * half + 2, :, :]
-                if share and half == 1:
+                if half in share:
                     nc.vector.tensor_copy(out=dst, in_=banks[half][:].rearrange("p i u r -> p i r u"))
                 else:
                     nc.scalar.copy(out=dst, in_=banks[half][:].rearrange("p i u r -> p i r u"))
@@ -230,7 +231,7 @@ def tile_groupqueryattention_pa_t_kernel(
             c_tiles[pg] = pair
 
         def front(gi):
-            state[gi] = {"grouped": transpose_group(x_sb[gi])}
+            state[gi] = {"grouped": transpose_group(x_sb[gi], share=VSHARE.get(gi, ()))}
 
         def table_front(pg, n):
             if n == 0:
@@ -370,20 +371,20 @@ def tile_groupqueryattention_pa_t_kernel(
             table_g2(eng, pg, n0, n1, 0)
             table_g2(eng, pg, n0, n1, 1)
 
-        late_tables = {0: (2, 0), 1: (2, 1), 3: (2, 2), 5: (2, 3)}
+        late_tables = {4: (2, 0), 5: (2, 1), 6: (2, 2), 7: (2, 3)}
         all_blocks = [(n, h) for n in range(NT) for h in range(NH)]
         vector_blocks = all_blocks
 
-        table_tile(nc.vector, 0, 0, NT)
-        w_grouped = transpose_group(w_sb)
+        table_tile(nc.vector, 0, 0, 2)
+        w_grouped = transpose_group(w_sb, pool=psum_u, tag="u")
         for n in range(2):
             table_tile(nc.gpsimd, 1, n, n + 1)
         quantise(w_grouped, w_codes, w_scales)
         for it in range(-2, NG + 1):
             if it + 2 < NG:
                 front(it + 2)
-            if it == -2:
-                table_t(0, psum_u, "u")
+            if it == 0:
+                table_c(0)
             if it in late_tables:
                 pg, n = late_tables[it]
                 wide = table_front(pg, n)
@@ -422,9 +423,12 @@ def tile_groupqueryattention_pa_t_kernel(
                 pg, b = order[it - 1]
                 if b == B - 1 and pg + 1 < PG:
                     table_c(pg + 1)
+            if it == -2:
+                table_tile(nc.vector, 0, 2, NT)
             if it == -1:
-                table_c(0)
-            if it == 2 or it == 7:
+                small_tables()
+                table_t(0, psum_t, "xt")
+            if it == 2 or it == 8:
                 table_t(1 if it == 2 else 3, psum_t, "xt")
             if it - 1 == NG - 1:
                 join(nc.vector, it - 1, 2, NT)

@@ -427,7 +427,7 @@ def tile_groupqueryattention_pa_t_kernel(
                 table_tile(nc.vector, 0, 2, NT)
             if it == -1:
                 small_tables()
-                table_t(0, psum_t, "xt")
+                table_t(0, psum_c, "c")
             if it == 2 or it == 8:
                 table_t(1 if it == 2 else 3, psum_t, "xt")
             if it - 1 == NG - 1:

@@ -18,8 +18,10 @@ HALF = DH // 2
 NT = 4
 GROUP = P * NT
 PG = S // GROUP
+NQ = 2
 NH = 3
-VSHARE = {0: (1,), 1: (1,)}
+KEY = 2
+VAL = 3
 EPS = 1e-6
 FLOPS = 2 * B * S * D * 512
 
@@ -31,19 +33,23 @@ def tile_groupqueryattention_pa_t_kernel(
     with ExitStack() as ctx:
         const = ctx.enter_context(tc.tile_pool(name="const", bufs=1))
         xpool = ctx.enter_context(tc.tile_pool(name="xpool", bufs=1))
-        tabs = ctx.enter_context(tc.tile_pool(name="tabs", bufs=1))
         work = ctx.enter_context(tc.tile_pool(name="work", bufs=2))
         deep = ctx.enter_context(tc.tile_pool(name="deep", bufs=3))
+        prods = ctx.enter_context(tc.tile_pool(name="prods", bufs=5))
         single = ctx.enter_context(tc.tile_pool(name="single", bufs=1))
         psum_t = ctx.enter_context(tc.psum_pool(name="psum_t", bufs=2))
-        psum_u = ctx.enter_context(tc.psum_pool(name="psum_u", bufs=4))
-        psum_c = ctx.enter_context(tc.psum_pool(name="psum_c", bufs=2))
+        psum_q = ctx.enter_context(tc.psum_pool(name="psum_q", bufs=2))
+        psum_s = ctx.enter_context(tc.psum_pool(name="psum_s", bufs=1))
         ctx.enter_context(tc.manual_schedule())
 
         order = [(pg, b) for pg in range(PG) for b in range(B)]
+        NG = len(order)
 
         ident_f = const.tile([P, P], F32, name="ident_f")
         make_identity(nc, ident_f[:])
+        x_sb = []
+        cs = []
+        sn = []
 
         def load_x(gi):
             pg, b = order[gi]
@@ -54,114 +60,103 @@ def tile_groupqueryattention_pa_t_kernel(
             )
             x_sb.append(xs)
 
-        def load_cs(eng, pg):
-            for c, tab in enumerate((cos_thetas, sin_thetas)):
-                eng.dma_start(
-                    out=cs_sb[:, c, pg * NT:(pg + 1) * NT, :],
-                    in_=tab[pg * GROUP:(pg + 1) * GROUP, :].rearrange("(p n) j -> p n j", n=NT),
-                )
+        def load_cs(pg):
+            cst_in = const.tile([P, 2, NT, DH], BF16, name="cs%d" % pg)
+            snt = const.tile([P, NT, 2, HALF], BF16, name="sn%d" % pg)
+            nc.sync.dma_start(
+                out=cst_in[:, 0, :, :].rearrange("p n j -> p (n j)"),
+                in_=cos_thetas[pg * GROUP:(pg + 1) * GROUP, :].rearrange("(p n) j -> p (n j)", n=NT),
+            )
+            nc.sync.dma_start(
+                out=snt[:].rearrange("p n c j -> p (n c j)"),
+                in_=sin_thetas[pg * GROUP:(pg + 1) * GROUP, :].rearrange("(p n) j -> p (n j)", n=NT),
+            )
+            cs.append(cst_in)
+            sn.append(snt)
 
-        x_sb = []
         w_sb = const.tile([P, NT, D], BF16, name="w_sb")
         vrow = const.tile([P, 4, DH], BF16, name="vrow")
         nc.vector.memset(vrow[:], 0.0)
         ones_b = const.tile([P, P], BF16, name="ones_b")
         nc.vector.memset(ones_b[:], 1.0)
         vectors = (q_scale, k_scale, q_shift, k_shift)
-
         vload = const.tile([1, 4, DH], BF16, name="vload")
-
-        def load_vector(i):
-            nc.sync.dma_start(out=vload[0:1, i, :], in_=vectors[i].rearrange("(o j) -> o j", o=1))
-
-        def spread_vectors(i0):
-            spread = psum_c.tile([P, 2, DH], F32, tag="c", name="spread")
-            nc.tensor.matmul(
-                spread[:].rearrange("p i j -> p (i j)"), lhsT=ones_b[:],
-                rhs=vrow[:, i0:i0 + 2, :].rearrange("p i j -> p (i j)"), start=True, stop=True,
-            )
-            return spread
-
-        cs_sb = const.tile([P, 2, PG * NT, DH], BF16, name="cs_sb")
         for i in range(4):
-            load_vector(i)
-        nc.vector.tensor_copy(out=vrow[0:1, :, :], in_=vload[:])
-        load_cs(nc.sync, 0)
-        load_cs(nc.sync, 1)
+            nc.sync.dma_start(out=vload[0:1, i, :], in_=vectors[i].rearrange("(o j) -> o j", o=1))
+        load_cs(0)
         nc.sync.dma_start(out=w_sb[:, 0:2, :], in_=wq.rearrange("(r p) k -> p r k", p=P))
-        nc.sync.dma_start(out=w_sb[:, 2, :], in_=wk)
-        nc.sync.dma_start(out=w_sb[:, 3, :], in_=wv)
+        nc.sync.dma_start(out=w_sb[:, KEY, :], in_=wk)
+        nc.sync.dma_start(out=w_sb[:, VAL, :], in_=wv)
         load_x(0)
+        load_cs(1)
         load_x(1)
         load_x(2)
         load_x(3)
-        load_cs(nc.sync, 2)
+        load_cs(2)
         load_x(4)
         load_x(5)
-        load_cs(nc.sync, 3)
-        for gi in range(6, len(order)):
+        load_cs(3)
+        for gi in range(6, NG):
             load_x(gi)
 
+        nc.vector.tensor_copy(out=vrow[0:1, :, :], in_=vload[:])
         eps_t = const.tile([P, 1], F32, name="eps_t")
         nc.vector.memset(eps_t[:], EPS)
         warm = const.tile([P, 1], F32, name="warm")
         nc.scalar.activation(out=warm[:], in_=eps_t[:], func=ACT.Abs_reciprocal_sqrt)
-
         ident_b = const.tile([P, P], BF16, name="ident_b")
         nc.vector.tensor_copy(out=ident_b[:], in_=ident_f[:])
         perm_f = const.tile([P, P], F32, name="perm_f")
         nc.vector.tensor_copy(out=perm_f[:, 0:HALF], in_=ident_f[:, HALF:])
         nc.vector.tensor_copy(out=perm_f[:, HALF:], in_=ident_f[:, 0:HALF])
 
-        g3 = const.tile([P, NH, DH], F32, name="g3")
-        scales_ps = spread_vectors(0)
-        nc.vector.tensor_scalar_add(out=g3[:, 0:2, :], in0=scales_ps[:, 0:1, :].to_broadcast([P, 2, DH]), scalar1=1.0)
-        nc.vector.tensor_scalar_add(out=g3[:, 2, :], in0=scales_ps[:, 1, :], scalar1=1.0)
-        gs3 = const.tile([P, NH, DH], F32, name="gs3")
-        nc.vector.tensor_copy(out=gs3[:, :, 0:HALF], in_=g3[:, :, 0:HALF])
-        nc.vector.tensor_scalar_mul(out=gs3[:, :, HALF:], in0=g3[:, :, HALF:], scalar1=-1.0)
+        def spread_vectors(i0, tag):
+            spread = psum_s.tile([P, 2, DH], F32, tag=tag, name="spread")
+            nc.tensor.matmul(
+                spread[:].rearrange("p i j -> p (i j)"), lhsT=ones_b[:],
+                rhs=vrow[:, i0:i0 + 2, :].rearrange("p i j -> p (i j)"), start=True, stop=True,
+            )
+            return spread
 
+        gains = const.tile([P, 2, 2, DH], F32, name="gains")
+        scales_ps = spread_vectors(0, "kv")
+        nc.vector.tensor_scalar_add(out=gains[:, :, 0, :], in0=scales_ps[:], scalar1=1.0)
+        nc.vector.tensor_copy(out=gains[:, :, 1, 0:HALF], in_=gains[:, :, 0, 0:HALF])
+        nc.vector.tensor_scalar_mul(out=gains[:, :, 1, HALF:], in0=gains[:, :, 0, HALF:], scalar1=-1.0)
+        colv = const.tile([P, 2], F32, name="colv")
         dc = const.tile([P, 2, DH], BF16, name="dc")
         ds = const.tile([P, 2, DH], BF16, name="ds")
-        dg = const.tile([P, 2, 2, DH], F32, name="dg")
-        bsrc = const.tile([P, 4, DH], F32, name="bsrc")
-        colv = const.tile([P, 4], F32, name="colv")
 
-        def small_tables():
-            nc.vector.tensor_copy(out=bsrc[:, 0:2, :], in_=g3[:, 1:3, :])
-            nc.vector.tensor_copy(out=bsrc[:, 2:4, 0:HALF], in_=gs3[:, 1:3, HALF:])
-            nc.vector.tensor_copy(out=bsrc[:, 2:4, HALF:], in_=gs3[:, 1:3, 0:HALF])
-            shifts_ps = spread_vectors(2)
+        def key_gain_columns():
+            col_ps = psum_s.tile([P, 2, P], F32, tag="tk", name="col_ps")
+            for a in range(2):
+                nc.tensor.transpose(col_ps[:, a, :], gains[:, 1, a, :], ident_f[:])
+            nc.scalar.copy(out=colv[:], in_=col_ps[:, :, 0])
+
+        def shift_matrices():
+            shifts_ps = spread_vectors(2, "kT")
             nc.vector.tensor_tensor(
-                out=dc[:], in0=shifts_ps[:], in1=ident_b[:].unsqueeze(1).to_broadcast([P, 2, DH]), op=ALU.mult
+                out=dc[:], in0=shifts_ps[:], in1=ident_f[:].unsqueeze(1).to_broadcast([P, 2, DH]), op=ALU.mult
             )
             nc.vector.scalar_tensor_tensor(
                 out=ds[:, :, 0:HALF], in0=shifts_ps[:, :, HALF:], scalar=-1.0,
-                in1=ident_b[:, 0:HALF].unsqueeze(1).to_broadcast([P, 2, HALF]), op0=ALU.mult, op1=ALU.mult,
+                in1=perm_f[:, 0:HALF].unsqueeze(1).to_broadcast([P, 2, HALF]), op0=ALU.mult, op1=ALU.mult,
             )
             nc.vector.tensor_tensor(
                 out=ds[:, :, HALF:], in0=shifts_ps[:, :, 0:HALF],
-                in1=ident_b[:, HALF:].unsqueeze(1).to_broadcast([P, 2, HALF]), op=ALU.mult,
+                in1=perm_f[:, HALF:].unsqueeze(1).to_broadcast([P, 2, HALF]), op=ALU.mult,
             )
-            col_ps = psum_c.tile([P, 4, P], F32, tag="c", name="col_ps")
-            for i in range(4):
-                nc.tensor.transpose(col_ps[:, i, :], bsrc[:, i, :], ident_f[:])
-            nc.scalar.copy(out=colv[:], in_=col_ps[:, :, 0])
-            for i in range(4):
-                nc.scalar.activation(
-                    out=dg[:, i // 2, i % 2, :], in_=ident_f[:] if i < 2 else perm_f[:], func=ACT.Copy,
-                    scale=colv[:, i:i + 1],
-                )
 
-        NG = len(order)
         w_codes = const.tile([P, NT * P], U32, name="w_codes", align_bytes=64)
         w_scales = const.tile([P, NT * P], U8, name="w_scales", align_bytes=64)
         state = {}
-        g12_tiles = {}
+        qtab = {}
+        ktab = {}
         cst_tiles = {}
-        c_tiles = {}
+        cq_tiles = {}
+        ck_tiles = {}
 
-        def transpose_group(src, share=(), pool=psum_t, tag="xt"):
+        def transpose_group(src, share, pool, tag):
             grouped = work.tile([P, NT, P, 4], BF16, tag="grouped", name="grouped", align_bytes=64)
             gwords = grouped[:].bitcast(F32)
             banks = []
@@ -185,75 +180,55 @@ def tile_groupqueryattention_pa_t_kernel(
                 out=codes[:].bitcast(FP8X4), scales=scales[:], in_=grouped[:].rearrange("p n r t -> p (n r t)")
             )
 
-        def table_g1(eng, pg, n0, n1):
-            g12 = g12_tiles[pg]
-            k = n1 - n0
-            cosv = cs_sb[:, 0, pg * NT + n0:pg * NT + n1, :]
-            eng.tensor_tensor(
-                out=g12[:, n0:n1, 0, :, :], in0=cosv.unsqueeze(2).to_broadcast([P, k, NH, DH]),
-                in1=g3[:].unsqueeze(1).to_broadcast([P, k, NH, DH]), op=ALU.mult,
+        def swap_sin(pg):
+            nc.vector.tensor_copy(
+                out=cs[pg][:, 1, :, :].rearrange("p n (c j) -> p n c j", c=2), in_=sn[pg][:, :, ::-1, :]
             )
 
-        def table_g2(eng, pg, n0, n1, c):
-            g12 = g12_tiles[pg]
-            k = n1 - n0
-            sinv = cs_sb[:, 1, pg * NT + n0:pg * NT + n1, (1 - c) * HALF:(2 - c) * HALF]
+        def query_table(eng, pg, a0, a1):
+            if pg not in qtab:
+                qtab[pg] = const.tile([P, 2, NT, DH], F32, name="qtab%d" % pg)
             eng.tensor_tensor(
-                out=g12[:, n0:n1, 1, :, c * HALF:(c + 1) * HALF],
-                in0=sinv.unsqueeze(2).to_broadcast([P, k, NH, HALF]),
-                in1=gs3[:, :, c * HALF:(c + 1) * HALF].unsqueeze(1).to_broadcast([P, k, NH, HALF]), op=ALU.mult,
+                out=qtab[pg][:, a0:a1, :, :], in0=cs[pg][:, a0:a1, :, :],
+                in1=gains[:, 0, a0:a1, :].unsqueeze(2).to_broadcast([P, a1 - a0, NT, DH]), op=ALU.mult,
             )
 
-        def table_t(pg, pool, tag):
+        def transpose_table(pg, pool, tag):
             cst_ps = pool.tile([P, 2, NT, P], BF16, tag=tag, name="cst_ps")
             for c in range(2):
                 for n in range(NT):
-                    nc.tensor.transpose(cst_ps[:, c, n, :], cs_sb[:, c, pg * NT + n, :], ident_b[:])
+                    nc.tensor.transpose(cst_ps[:, c, n, :], cs[pg][:, c, n, :], ident_b[:])
             cst = work.tile([P, 2, NT, P], BF16, tag="cst", name="cst")
             nc.scalar.copy(out=cst[:], in_=cst_ps[:])
             cst_tiles[pg] = cst
 
-        def table_c(pg):
+        def key_table(pg, a):
+            if a == 0:
+                ktab[pg] = work.tile([P, 2, GROUP], F32, tag="ktab", name="ktab")
+            nc.scalar.activation(
+                out=ktab[pg][:, a, :], in_=cst_tiles[pg][:, a, :, :].rearrange("p n r -> p (n r)"), func=ACT.Copy,
+                scale=colv[:, a:a + 1],
+            )
+
+        def shift_table(pg, kind, tag):
             cst = cst_tiles[pg]
-            pair = []
-            for half in range(2):
-                c_ps = psum_c.tile([P, 2, 2, DH], F32, tag="c", name="c_ps")
-                for i in range(2):
-                    n = 2 * half + i
-                    dst = c_ps[:, i, :, :].rearrange("p a j -> p (a j)")
-                    nc.tensor.matmul(
-                        dst, lhsT=cst[:, 0, n, :], rhs=dc[:].rearrange("p a j -> p (a j)"), start=True, stop=False
-                    )
-                    nc.tensor.matmul(
-                        dst, lhsT=cst[:, 1, n, :], rhs=ds[:].rearrange("p a j -> p (a j)"), start=False, stop=True
-                    )
-                pair.append(c_ps)
-            c_tiles[pg] = pair
+            c_ps = psum_s.tile([P, NT, DH], F32, tag=tag, name="c_ps")
+            for n in range(NT):
+                nc.tensor.matmul(c_ps[:, n, :], lhsT=cst[:, 0, n, :], rhs=dc[:, kind, :], start=True, stop=False)
+                nc.tensor.matmul(c_ps[:, n, :], lhsT=cst[:, 1, n, :], rhs=ds[:, kind, :], start=False, stop=True)
+            return c_ps
 
-        def front(gi):
-            state[gi] = {"grouped": transpose_group(x_sb[gi], share=VSHARE.get(gi, ()))}
+        def key_shift(pg):
+            c_ps = shift_table(pg, 1, "kv")
+            ck = work.tile([P, NT, DH], F32, tag="ck", name="ck")
+            nc.scalar.copy(out=ck[:], in_=c_ps[:])
+            ck_tiles[pg] = ck
 
-        def table_front(pg, n):
-            if n == 0:
-                cst_tiles[pg] = work.tile([P, 2, NT, P], BF16, tag="cst", name="cst")
-            cs_ps = psum_t.tile([P, 2, P], BF16, tag="xt", name="cs_ps")
-            for c in range(2):
-                nc.tensor.transpose(cs_ps[:, c, :], cs_sb[:, c, pg * NT + n, :], ident_b[:])
-            nc.scalar.copy(out=cst_tiles[pg][:, :, n, :], in_=cs_ps[:])
-            csf = work.tile([P, 2, P], F32, tag="csf", name="csf")
-            nc.scalar.copy(out=csf[:], in_=cs_ps[:])
-            return csf
+        def query_shift(pg):
+            cq_tiles[pg] = shift_table(pg, 0, "c")
 
-        def table_back(pg, n, csf):
-            gt = psum_t.tile([P, 2, 2, P], F32, tag="xt", name="gt")
-            for a in range(2):
-                nc.tensor.matmul(
-                    gt[:, a, :, :].rearrange("p q j -> p (q j)"), lhsT=csf[:, a, :],
-                    rhs=dg[:, a, :, :].rearrange("p q j -> p (q j)"), start=True, stop=True,
-                )
-            g12 = g12_tiles[pg]
-            nc.scalar.copy(out=g12[:, n, :, 0:2, :], in_=gt[:, :, 0:1, :].to_broadcast([P, 2, 2, DH]))
-            nc.scalar.copy(out=g12[:, n, :, 2, :], in_=gt[:, :, 1, :])
+        def front(gi, share=()):
+            state[gi] = {"grouped": transpose_group(x_sb[gi], share, psum_t, "xt")}
 
         def quant(gi):
             st = state[gi]
@@ -261,177 +236,234 @@ def tile_groupqueryattention_pa_t_kernel(
             st["scales"] = deep.tile([P, NT * P], U8, tag="scales", name="scales", align_bytes=64)
             quantise(st["grouped"], st["codes"], st["scales"])
 
-        def project(gi, n):
+        def project(gi, row, bank):
             st = state[gi]
-            if n == 0:
-                st["ss"] = deep.tile([P, NT * NH], F32, tag="ss", name="ss")
-                st["ov"] = deep.tile([P, NT, DH], F32, tag="ov", name="ov")
-                st["u"] = []
-            codes, scales, ss, ov = st["codes"], st["scales"], st["ss"], st["ov"]
-            u = psum_u.tile([P, 4 * DH], F32, tag="u", name="u")
-            st["u"].append(u)
+            for n in range(NT):
+                nc.tensor.matmul_mx(
+                    out=bank[:, n, :],
+                    lhsT=st["codes"][:, n * P:(n + 1) * P].bitcast(FP8X4),
+                    lhsT_scale=st["scales"][:, n * P:(n + 1) * P],
+                    rhs=w_codes[:, row * P:(row + 1) * P].bitcast(FP8X4),
+                    rhs_scale=w_scales[:, row * P:(row + 1) * P],
+                    start=True,
+                    stop=True,
+                )
+
+        def squares(gi, h, bank):
+            st = state[gi]
+            if "ss" not in st:
+                st["ss"] = deep.tile([P, NH * NT], F32, tag="ss", name="ss")
+            for n in range(NT):
+                junk = work.tile([P, DH], BF16, tag="junk", name="junk")
+                nc.scalar.activation(
+                    out=junk[:], in_=bank[:, n, :], func=ACT.Square,
+                    accum_out=st["ss"][:, h * NT + n:h * NT + n + 1],
+                )
+
+        def project_key(gi):
+            bank = psum_s.tile([P, NT, DH], F32, tag="kv", name="kbank")
+            project(gi, KEY, bank)
+            squares(gi, KEY, bank)
+
+        def project_key_t(gi):
+            st = state[gi]
+            st["kT"] = psum_s.tile([P, GROUP], F32, tag="kT", name="kT")
             nc.tensor.matmul_mx(
-                out=u[:],
-                lhsT=codes[:, n * P:(n + 1) * P].bitcast(FP8X4),
-                lhsT_scale=scales[:, n * P:(n + 1) * P],
-                rhs=w_codes[:].bitcast(FP8X4),
-                rhs_scale=w_scales[:],
+                out=st["kT"][:],
+                lhsT=w_codes[:, KEY * P:(KEY + 1) * P].bitcast(FP8X4),
+                lhsT_scale=w_scales[:, KEY * P:(KEY + 1) * P],
+                rhs=st["codes"][:].bitcast(FP8X4),
+                rhs_scale=st["scales"][:],
                 start=True,
                 stop=True,
             )
-            for h in range(NH):
-                junk = work.tile([P, DH], BF16, tag="junk", name="junk")
-                nc.scalar.activation(
-                    out=junk[:], in_=u[:, h * DH:(h + 1) * DH], func=ACT.Square,
-                    accum_out=ss[:, n * NH + h:n * NH + h + 1],
-                )
-            nc.scalar.copy(out=ov[:, n, :], in_=u[:, NH * DH:])
 
-        def norm_root(gi):
+        def project_value(gi):
             pg, b = order[gi]
-            st = state[gi]
-            st["rinv"] = deep.tile([P, NT * NH], F32, tag="rinv", name="rinv")
-            nc.scalar.activation(
-                out=st["rinv"][:], in_=st["ss"][:], func=ACT.Abs_reciprocal_sqrt, scale=1.0 / DH, bias=eps_t[:]
-            )
+            bank = psum_s.tile([P, NT, DH], F32, tag="kv", name="vbank")
+            project(gi, VAL, bank)
+            ov = deep.tile([P, NT, DH], F32, tag="ov", name="ov")
+            nc.scalar.copy(out=ov[:], in_=bank[:])
             lo = pg * GROUP
             nc.sync.dma_start(
                 out=out_2[b, 0, lo:lo + GROUP, :].rearrange("(p n) j -> p (n j)", n=NT),
-                in_=st["ov"][:].rearrange("p n j -> p (n j)"),
+                in_=ov[:].rearrange("p n j -> p (n j)"),
             )
 
-        def products(gi, n):
+        def project_query(gi, h):
+            st = state[gi]
+            bank = psum_q.tile([P, NT, DH], F32, tag="q", name="qbank")
+            st["q%d" % h] = bank
+            project(gi, h, bank)
+            squares(gi, h, bank)
+
+        def norm_root(gi):
+            st = state[gi]
+            st["rinv"] = deep.tile([P, NH * NT], F32, tag="rinv", name="rinv")
+            nc.scalar.activation(
+                out=st["rinv"][:], in_=st["ss"][:], func=ACT.Abs_reciprocal_sqrt, scale=1.0 / DH, bias=eps_t[:]
+            )
+
+        def products_key(gi):
             pg, b = order[gi]
             st = state[gi]
-            if n == 0:
-                st["t12"] = deep.tile([P, 2, NT, NH, 2, HALF], F32, tag="t12", name="t12")
-            u = st["u"][n]
+            st["pk"] = work.tile([P, 2, GROUP], F32, tag="pk", name="pk")
             nc.vector.tensor_tensor(
-                out=st["t12"][:, :, n, :, :, :].rearrange("p a h c j -> p a (h c j)"),
-                in0=u[:, 0:NH * DH].unsqueeze(1).to_broadcast([P, 2, NH * DH]),
-                in1=g12_tiles[pg][:, n, :, :, :].rearrange("p a h j -> p a (h j)"),
+                out=st["pk"][:], in0=st["kT"][:].unsqueeze(1).to_broadcast([P, 2, GROUP]), in1=ktab[pg][:], op=ALU.mult
+            )
+
+        def products_query(gi, h):
+            pg, b = order[gi]
+            st = state[gi]
+            t12 = prods.tile([P, 2, NT, 2, HALF], F32, tag="t12", name="t12")
+            st["t%d" % h] = t12
+            nc.vector.tensor_tensor(
+                out=t12[:].rearrange("p a n c j -> p a (n c j)"),
+                in0=st["q%d" % h][:].rearrange("p n j -> p (n j)").unsqueeze(1).to_broadcast([P, 2, NT * DH]),
+                in1=qtab[pg][:].rearrange("p a n j -> p a (n j)"),
                 op=ALU.mult,
             )
 
-        def join(eng, gi, n0, n1):
-            t12 = state[gi]["t12"]
-            for c in range(2):
-                eng.tensor_tensor(
-                    out=t12[:, 0, n0:n1, :, c, :], in0=t12[:, 0, n0:n1, :, c, :],
-                    in1=t12[:, 1, n0:n1, :, 1 - c, :], op=ALU.add,
-                )
+        def join_key(gi):
+            st = state[gi]
+            tk = psum_s.tile([P, NT, DH], F32, tag="tk", name="tk")
+            for n in range(NT):
+                for a, moving in ((0, ident_f), (1, perm_f)):
+                    nc.tensor.matmul(
+                        tk[:, n, :], lhsT=st["pk"][:, a, n * P:(n + 1) * P], rhs=moving[:],
+                        start=a == 0, stop=a == 1, is_transpose=True,
+                    )
+            st["tk"] = tk
+
+        def scale_key(gi):
+            st = state[gi]
+            ks = work.tile([P, NT, DH], F32, tag="ks", name="ks")
+            for n in range(NT):
+                i = KEY * NT + n
+                nc.scalar.activation(out=ks[:, n, :], in_=st["tk"][:, n, :], func=ACT.Copy, scale=st["rinv"][:, i:i + 1])
+            st["ks"] = ks
+
+        def finish_key(gi):
+            pg, b = order[gi]
+            st = state[gi]
+            ok = deep.tile([P, NT, DH], F32, tag="ok", name="ok")
+            nc.gpsimd.tensor_tensor(out=ok[:], in0=st["ks"][:], in1=ck_tiles[pg][:], op=ALU.add)
+            lo = pg * GROUP
+            nc.sync.dma_start(
+                out=out_1[b, 0, lo:lo + GROUP, :].rearrange("(p n) j -> p (n j)", n=NT),
+                in_=ok[:].rearrange("p n j -> p (n j)"),
+            )
+
+        def join_query(eng, gi, h, dst):
+            t12 = state[gi]["t%d" % h]
+            eng.tensor_tensor(out=dst, in0=t12[:, 0, :, :, :], in1=t12[:, 1, :, ::-1, :], op=ALU.add)
 
         def join_pool(gi):
-            st = state[gi]
-            t12 = st["t12"]
-            t3 = single.tile([P, NT, NH, 2, HALF], F32, tag="t3", name="t3")
-            st["t3"] = t3
-            for n0 in (0, 2):
-                nc.gpsimd.tensor_tensor(
-                    out=t3[:, n0:n0 + 2, :, :, :].rearrange("p n h c j -> p (n h) c j"),
-                    in0=t12[:, 0, n0:n0 + 2, :, :, :].rearrange("p n h c j -> p (n h) c j"),
-                    in1=t12[:, 1, n0:n0 + 2, :, :, :].rearrange("p n h c j -> p (n h) c j")[:, :, ::-1, :],
-                    op=ALU.add,
-                )
+            t3 = single.tile([P, NQ, NT, 2, HALF], F32, tag="t3", name="t3")
+            for h in range(NQ):
+                join_query(nc.gpsimd, gi, h, t3[:, h, :, :, :])
+            state[gi]["sums"] = [t3[:, h, :, :, :] for h in range(NQ)]
 
         def finish(gi, blocks):
             pg, b = order[gi]
             st = state[gi]
-            if "oqk" not in st:
-                st["oqk"] = deep.tile([P, NH, NT, DH], F32, tag="oqk", name="oqk")
-            for n, h in blocks:
-                summed = st["t3"][:, n, h, :, :] if "t3" in st else st["t12"][:, 0, n, h, :, :]
+            if "oq" not in st:
+                st["oq"] = deep.tile([P, NQ, NT, DH], F32, tag="oq", name="oq")
+            for h, n in blocks:
+                i = h * NT + n
                 nc.vector.scalar_tensor_tensor(
-                    out=st["oqk"][:, h, n, :],
-                    in0=summed.rearrange("p c j -> p (c j)"),
-                    scalar=st["rinv"][:, n * NH + h:n * NH + h + 1],
-                    in1=c_tiles[pg][n // 2][:, n % 2, h // 2, :],
+                    out=st["oq"][:, h, n, :],
+                    in0=st["sums"][h][:, n, :, :].rearrange("p c j -> p (c j)"),
+                    scalar=st["rinv"][:, i:i + 1],
+                    in1=cq_tiles[pg][:, n, :],
                     op0=ALU.mult,
                     op1=ALU.add,
                 )
 
-        def store(gi, n0, n1):
+        def store(gi, h0, h1):
             pg, b = order[gi]
-            oqk = state[gi]["oqk"]
             lo = pg * GROUP
             nc.sync.dma_start(
-                out=out_0[b, :, lo:lo + GROUP, :].rearrange("h (p n) j -> p h n j", n=NT)[:, :, n0:n1, :],
-                in_=oqk[:, 0:2, n0:n1, :],
-            )
-            nc.sync.dma_start(
-                out=out_1[b, 0, lo:lo + GROUP, :].rearrange("(p n) j -> p n j", n=NT)[:, n0:n1, :],
-                in_=oqk[:, 2, n0:n1, :],
+                out=out_0[b, h0:h1, lo:lo + GROUP, :].rearrange("h (p n) j -> p h (n j)", n=NT),
+                in_=state[gi]["oq"][:, h0:h1, :, :].rearrange("p h n j -> p h (n j)"),
             )
 
-        for pg in range(PG):
-            g12_tiles[pg] = tabs.tile([P, NT, 2, NH, DH], F32, name="g12_%d" % pg)
-
-        def table_tile(eng, pg, n0, n1):
-            table_g1(eng, pg, n0, n1)
-            table_g2(eng, pg, n0, n1, 0)
-            table_g2(eng, pg, n0, n1, 1)
-
-        late_tables = {4: (2, 0), 5: (2, 1), 6: (2, 2), 7: (2, 3)}
-        all_blocks = [(n, h) for n in range(NT) for h in range(NH)]
-        vector_blocks = all_blocks
-
-        table_tile(nc.vector, 0, 0, 2)
-        w_grouped = transpose_group(w_sb, pool=psum_u, tag="u")
-        for n in range(2):
-            table_tile(nc.gpsimd, 1, n, n + 1)
+        all_blocks = [(h, n) for h in range(NQ) for n in range(NT)]
+        key_gain_columns()
+        swap_sin(0)
+        w_grouped = transpose_group(w_sb, (1,), psum_q, "q")
+        query_table(nc.vector, 0, 0, 2)
         quantise(w_grouped, w_codes, w_scales)
+        transpose_table(0, psum_s, "c")
         for it in range(-2, NG + 1):
+            last = it == NG - 1
             if it + 2 < NG:
-                front(it + 2)
-            if it == 0:
-                table_c(0)
-            if it in late_tables:
-                pg, n = late_tables[it]
-                wide = table_front(pg, n)
+                front(it + 2, (1,) if it < 0 else ())
             if 0 <= it - 1 < NG - 1:
                 join_pool(it - 1)
-            if it == 1 or it == 2:
-                table_tile(nc.gpsimd, 1, it + 1, it + 2)
-            if 4 <= it < 4 + 2 * NT:
-                n = (it - 4) // 2
-                if it % 2 == 0:
-                    table_g1(nc.gpsimd, 3, n, n + 1)
-                else:
-                    table_g2(nc.gpsimd, 3, n, n + 1, 0)
-                    table_g2(nc.gpsimd, 3, n, n + 1, 1)
-            for n in range(NT):
+            if 0 <= it < NG:
+                products_key(it)
+            if 0 <= it + 1 < NG:
+                project_key(it + 1)
+                project_key_t(it + 1)
+            if 0 <= it < NG:
+                join_key(it)
+                scale_key(it)
+                finish_key(it)
+            if 0 <= it + 1 < NG:
+                project_value(it + 1)
+            for h in range(NQ):
                 if 0 <= it < NG:
-                    products(it, n)
-                if it == 0 and n == 0:
-                    quant(1)
+                    products_query(it, h)
                 if 0 <= it + 1 < NG:
-                    project(it + 1, n)
-                if it == NG - 1 and n == 1:
-                    join(nc.gpsimd, it, 0, 2)
+                    project_query(it + 1, h)
+                if B < it < NG and it % B == 1 and h == 0:
+                    query_shift(it // B)
+                if last and h == 0:
+                    join_query(nc.gpsimd, it, 0, state[it]["t0"][:, 0, :, :, :])
             if 0 <= it + 1 < NG:
                 norm_root(it + 1)
-            if it in late_tables:
-                pg, n = late_tables[it]
-                table_back(pg, n, wide)
+            if it == -2:
+                quant(0)
+                shift_matrices()
+                key_table(0, 0)
+                key_table(0, 1)
+                swap_sin(1)
+                for a in range(2):
+                    query_table(nc.gpsimd, 1, a, a + 1)
+            elif it + 2 < NG and it < 0:
+                quant(it + 2)
+            if it == -1:
+                key_shift(0)
+                query_shift(0)
             if 0 <= it - 1 < NG - 1:
-                finish(it - 1, (vector_blocks if it - 1 >= 2 else all_blocks)[:-1])
-            if it + 2 < NG and it != -1:
+                finish(it - 1, all_blocks[:-1])
+            if it >= 0 and it + 2 < NG:
                 quant(it + 2)
             if 0 <= it - 1 < NG - 1:
-                finish(it - 1, vector_blocks[-1:])
-                store(it - 1, 0, NT)
-                pg, b = order[it - 1]
-                if b == B - 1 and pg + 1 < PG:
-                    table_c(pg + 1)
-            if it == -2:
-                table_tile(nc.vector, 0, 2, NT)
-            if it == -1:
-                small_tables()
-                table_t(0, psum_c, "c")
-            if it == 2 or it == 8:
-                table_t(1 if it == 2 else 3, psum_t, "xt")
-            if it - 1 == NG - 1:
-                join(nc.vector, it - 1, 2, NT)
-                for n0 in (2, 0):
-                    finish(it - 1, all_blocks[n0 * NH:(n0 + 2) * NH])
-                    store(it - 1, n0, n0 + 2)
+                finish(it - 1, all_blocks[-1:])
+                store(it - 1, 0, NQ)
+            if 0 <= it and it // B + 1 < PG:
+                pg = it // B + 1
+                step = it % B
+                if step == 0:
+                    if pg > 1:
+                        swap_sin(pg)
+                    transpose_table(pg, psum_t, "xt")
+                elif step == 1:
+                    key_table(pg, 0)
+                    if pg > 1:
+                        query_table(nc.gpsimd, pg, 0, 1)
+                elif step == 2:
+                    key_table(pg, 1)
+                    if pg > 1:
+                        query_table(nc.gpsimd, pg, 1, 2)
+                else:
+                    key_shift(pg)
+            if it == NG:
+                gi = NG - 1
+                join_query(nc.vector, gi, 1, state[gi]["t1"][:, 0, :, :, :])
+                state[gi]["sums"] = [state[gi]["t%d" % h][:, 0, :, :, :] for h in range(NQ)]
+                for h in (1, 0):
+                    finish(gi, all_blocks[h * NT:(h + 1) * NT])
+                    store(gi, h, h + 1)

@@ -35,7 +35,7 @@ def tile_groupqueryattention_pa_t_kernel(
         xpool = ctx.enter_context(tc.tile_pool(name="xpool", bufs=1))
         work = ctx.enter_context(tc.tile_pool(name="work", bufs=2))
         deep = ctx.enter_context(tc.tile_pool(name="deep", bufs=3))
-        prods = ctx.enter_context(tc.tile_pool(name="prods", bufs=5))
+        prods = ctx.enter_context(tc.tile_pool(name="prods", bufs=3))
         single = ctx.enter_context(tc.tile_pool(name="single", bufs=1))
         psum_t = ctx.enter_context(tc.psum_pool(name="psum_t", bufs=2))
         psum_q = ctx.enter_context(tc.psum_pool(name="psum_q", bufs=2))
@@ -83,20 +83,17 @@ def tile_groupqueryattention_pa_t_kernel(
         vload = const.tile([1, 4, DH], BF16, name="vload")
         for i in range(4):
             nc.sync.dma_start(out=vload[0:1, i, :], in_=vectors[i].rearrange("(o j) -> o j", o=1))
-        load_cs(0)
         nc.sync.dma_start(out=w_sb[:, 0:2, :], in_=wq.rearrange("(r p) k -> p r k", p=P))
         nc.sync.dma_start(out=w_sb[:, KEY, :], in_=wk)
         nc.sync.dma_start(out=w_sb[:, VAL, :], in_=wv)
         load_x(0)
-        load_cs(1)
+        load_cs(0)
         load_x(1)
+        load_cs(1)
         load_x(2)
-        load_x(3)
         load_cs(2)
-        load_x(4)
-        load_x(5)
         load_cs(3)
-        for gi in range(6, NG):
+        for gi in range(3, NG):
             load_x(gi)
 
         nc.vector.tensor_copy(out=vrow[0:1, :, :], in_=vload[:])
@@ -118,33 +115,28 @@ def tile_groupqueryattention_pa_t_kernel(
             )
             return spread
 
-        gains = const.tile([P, 2, 2, DH], F32, name="gains")
+        gains = const.tile([P, 2, DH], F32, name="gains")
         scales_ps = spread_vectors(0, "kv")
-        nc.vector.tensor_scalar_add(out=gains[:, :, 0, :], in0=scales_ps[:], scalar1=1.0)
-        nc.vector.tensor_copy(out=gains[:, :, 1, 0:HALF], in_=gains[:, :, 0, 0:HALF])
-        nc.vector.tensor_scalar_mul(out=gains[:, :, 1, HALF:], in0=gains[:, :, 0, HALF:], scalar1=-1.0)
-        colv = const.tile([P, 2], F32, name="colv")
+        nc.vector.tensor_scalar_add(out=gains[:], in0=scales_ps[:], scalar1=1.0)
+        key_gain = const.tile([P, 1], F32, name="key_gain")
         dc = const.tile([P, 2, DH], BF16, name="dc")
         ds = const.tile([P, 2, DH], BF16, name="ds")
 
         def key_gain_columns():
-            col_ps = psum_s.tile([P, 2, P], F32, tag="tk", name="col_ps")
-            for a in range(2):
-                nc.tensor.transpose(col_ps[:, a, :], gains[:, 1, a, :], ident_f[:])
-            nc.scalar.copy(out=colv[:], in_=col_ps[:, :, 0])
+            col_ps = psum_s.tile([P, P], F32, tag="tk", name="col_ps")
+            nc.tensor.transpose(col_ps[:], gains[:, 1, :], ident_f[:])
+            nc.scalar.copy(out=key_gain[:], in_=col_ps[:, 0:1])
 
         def shift_matrices():
             shifts_ps = spread_vectors(2, "kT")
             nc.vector.tensor_tensor(
                 out=dc[:], in0=shifts_ps[:], in1=ident_f[:].unsqueeze(1).to_broadcast([P, 2, DH]), op=ALU.mult
             )
-            nc.vector.scalar_tensor_tensor(
-                out=ds[:, :, 0:HALF], in0=shifts_ps[:, :, HALF:], scalar=-1.0,
-                in1=perm_f[:, 0:HALF].unsqueeze(1).to_broadcast([P, 2, HALF]), op0=ALU.mult, op1=ALU.mult,
-            )
             nc.vector.tensor_tensor(
-                out=ds[:, :, HALF:], in0=shifts_ps[:, :, 0:HALF],
-                in1=perm_f[:, HALF:].unsqueeze(1).to_broadcast([P, 2, HALF]), op=ALU.mult,
+                out=ds[:].rearrange("p i (c j) -> p i c j", c=2),
+                in0=shifts_ps[:].rearrange("p i (c j) -> p i c j", c=2)[:, :, ::-1, :],
+                in1=perm_f[:].rearrange("p (c j) -> p c j", c=2).unsqueeze(1).to_broadcast([P, 2, 2, HALF]),
+                op=ALU.mult,
             )
 
         w_codes = const.tile([P, NT * P], U32, name="w_codes", align_bytes=64)
@@ -181,16 +173,15 @@ def tile_groupqueryattention_pa_t_kernel(
             )
 
         def swap_sin(pg):
-            nc.vector.tensor_copy(
-                out=cs[pg][:, 1, :, :].rearrange("p n (c j) -> p n c j", c=2), in_=sn[pg][:, :, ::-1, :]
-            )
+            nc.vector.tensor_copy(out=cs[pg][:, 1, :, 0:HALF], in_=sn[pg][:, :, 1, :])
+            nc.vector.tensor_scalar_mul(out=cs[pg][:, 1, :, HALF:], in0=sn[pg][:, :, 0, :], scalar1=-1.0)
 
         def query_table(eng, pg, a0, a1):
             if pg not in qtab:
                 qtab[pg] = const.tile([P, 2, NT, DH], F32, name="qtab%d" % pg)
             eng.tensor_tensor(
                 out=qtab[pg][:, a0:a1, :, :], in0=cs[pg][:, a0:a1, :, :],
-                in1=gains[:, 0, a0:a1, :].unsqueeze(2).to_broadcast([P, a1 - a0, NT, DH]), op=ALU.mult,
+                in1=gains[:, 0:1, :].unsqueeze(1).to_broadcast([P, a1 - a0, NT, DH]), op=ALU.mult,
             )
 
         def transpose_table(pg, pool, tag):
@@ -198,24 +189,20 @@ def tile_groupqueryattention_pa_t_kernel(
             for c in range(2):
                 for n in range(NT):
                     nc.tensor.transpose(cst_ps[:, c, n, :], cs[pg][:, c, n, :], ident_b[:])
-            cst = work.tile([P, 2, NT, P], BF16, tag="cst", name="cst")
-            nc.scalar.copy(out=cst[:], in_=cst_ps[:])
+            cst = const.tile([P, 2 * NT, P], BF16, name="cst%d" % pg)
+            nc.scalar.copy(out=cst[:], in_=cst_ps[:].rearrange("p c n r -> p (c n) r"))
             cst_tiles[pg] = cst
 
-        def key_table(pg, a):
-            if a == 0:
-                ktab[pg] = work.tile([P, 2, GROUP], F32, tag="ktab", name="ktab")
-            nc.scalar.activation(
-                out=ktab[pg][:, a, :], in_=cst_tiles[pg][:, a, :, :].rearrange("p n r -> p (n r)"), func=ACT.Copy,
-                scale=colv[:, a:a + 1],
-            )
+        def key_table(pg):
+            ktab[pg] = const.tile([P, 2 * NT, P], F32, name="ktab%d" % pg)
+            nc.vector.tensor_scalar_mul(out=ktab[pg][:], in0=cst_tiles[pg][:], scalar1=key_gain[:])
 
         def shift_table(pg, kind, tag):
             cst = cst_tiles[pg]
             c_ps = psum_s.tile([P, NT, DH], F32, tag=tag, name="c_ps")
             for n in range(NT):
-                nc.tensor.matmul(c_ps[:, n, :], lhsT=cst[:, 0, n, :], rhs=dc[:, kind, :], start=True, stop=False)
-                nc.tensor.matmul(c_ps[:, n, :], lhsT=cst[:, 1, n, :], rhs=ds[:, kind, :], start=False, stop=True)
+                nc.tensor.matmul(c_ps[:, n, :], lhsT=cst[:, n, :], rhs=dc[:, kind, :], start=True, stop=False)
+                nc.tensor.matmul(c_ps[:, n, :], lhsT=cst[:, NT + n, :], rhs=ds[:, kind, :], start=False, stop=True)
             return c_ps
 
         def key_shift(pg):
@@ -309,16 +296,17 @@ def tile_groupqueryattention_pa_t_kernel(
             st = state[gi]
             st["pk"] = work.tile([P, 2, GROUP], F32, tag="pk", name="pk")
             nc.vector.tensor_tensor(
-                out=st["pk"][:], in0=st["kT"][:].unsqueeze(1).to_broadcast([P, 2, GROUP]), in1=ktab[pg][:], op=ALU.mult
+                out=st["pk"][:], in0=st["kT"][:].unsqueeze(1).to_broadcast([P, 2, GROUP]),
+                in1=ktab[pg][:].rearrange("p (a n) r -> p a (n r)", a=2), op=ALU.mult,
             )
 
         def products_query(gi, h):
             pg, b = order[gi]
             st = state[gi]
-            t12 = prods.tile([P, 2, NT, 2, HALF], F32, tag="t12", name="t12")
-            st["t%d" % h] = t12
+            if h == 0:
+                st["t12"] = prods.tile([P, 2, NQ, NT, 2, HALF], F32, tag="t12", name="t12")
             nc.vector.tensor_tensor(
-                out=t12[:].rearrange("p a n c j -> p a (n c j)"),
+                out=st["t12"][:, :, h, :, :, :].rearrange("p a n c j -> p a (n c j)"),
                 in0=st["q%d" % h][:].rearrange("p n j -> p (n j)").unsqueeze(1).to_broadcast([P, 2, NT * DH]),
                 in1=qtab[pg][:].rearrange("p a n j -> p a (n j)"),
                 op=ALU.mult,
@@ -354,15 +342,19 @@ def tile_groupqueryattention_pa_t_kernel(
                 in_=ok[:].rearrange("p n j -> p (n j)"),
             )
 
-        def join_query(eng, gi, h, dst):
-            t12 = state[gi]["t%d" % h]
-            eng.tensor_tensor(out=dst, in0=t12[:, 0, :, :, :], in1=t12[:, 1, :, ::-1, :], op=ALU.add)
+        def join_query(eng, gi, h0, h1, dst):
+            t12 = state[gi]["t12"]
+            eng.tensor_tensor(
+                out=dst.rearrange("p h n c j -> p (h n) c j"),
+                in0=t12[:, 0, h0:h1, :, :, :].rearrange("p h n c j -> p (h n) c j"),
+                in1=t12[:, 1, h0:h1, :, :, :].rearrange("p h n c j -> p (h n) c j")[:, :, ::-1, :],
+                op=ALU.add,
+            )
 
         def join_pool(gi):
             t3 = single.tile([P, NQ, NT, 2, HALF], F32, tag="t3", name="t3")
-            for h in range(NQ):
-                join_query(nc.gpsimd, gi, h, t3[:, h, :, :, :])
-            state[gi]["sums"] = [t3[:, h, :, :, :] for h in range(NQ)]
+            join_query(nc.gpsimd, gi, 0, NQ, t3[:])
+            state[gi]["sums"] = t3
 
         def finish(gi, blocks):
             pg, b = order[gi]
@@ -373,7 +365,7 @@ def tile_groupqueryattention_pa_t_kernel(
                 i = h * NT + n
                 nc.vector.scalar_tensor_tensor(
                     out=st["oq"][:, h, n, :],
-                    in0=st["sums"][h][:, n, :, :].rearrange("p c j -> p (c j)"),
+                    in0=st["sums"][:, h, n, :, :].rearrange("p c j -> p (c j)"),
                     scalar=st["rinv"][:, i:i + 1],
                     in1=cq_tiles[pg][:, n, :],
                     op0=ALU.mult,
@@ -390,80 +382,84 @@ def tile_groupqueryattention_pa_t_kernel(
 
         all_blocks = [(h, n) for h in range(NQ) for n in range(NT)]
         key_gain_columns()
-        swap_sin(0)
         w_grouped = transpose_group(w_sb, (1,), psum_q, "q")
-        query_table(nc.vector, 0, 0, 2)
         quantise(w_grouped, w_codes, w_scales)
+        front(0, (1,))
+        swap_sin(0)
+        quant(0)
+        query_table(nc.vector, 0, 0, 2)
+        front(1)
         transpose_table(0, psum_s, "c")
-        for it in range(-2, NG + 1):
+        quant(1)
+        shift_matrices()
+        for h in range(NQ):
+            project_query(0, h)
+        key_table(0)
+        front(2)
+        project_key(0)
+        project_key_t(0)
+        project_value(0)
+        norm_root(0)
+        swap_sin(1)
+        for a in range(2):
+            query_table(nc.gpsimd, 1, a, a + 1)
+        for it in range(NG + 1):
             last = it == NG - 1
-            if it + 2 < NG:
-                front(it + 2, (1,) if it < 0 else ())
             if 0 <= it - 1 < NG - 1:
                 join_pool(it - 1)
-            if 0 <= it < NG:
-                products_key(it)
-            if 0 <= it + 1 < NG:
+            if 0 <= it - 1 < NG:
+                finish_key(it - 1)
+            if B < it < NG and it % B == 1:
+                query_shift(it // B)
+            if it < NG:
+                products_query(it, 0)
+            if it + 1 < NG:
+                project_query(it + 1, 0)
+            if it + 1 < NG:
                 project_key(it + 1)
-                project_key_t(it + 1)
-            if 0 <= it < NG:
-                join_key(it)
-                scale_key(it)
-                finish_key(it)
-            if 0 <= it + 1 < NG:
+            if it < NG:
+                products_query(it, 1)
+            if it + 1 < NG:
+                project_query(it + 1, 1)
+            if last:
+                join_query(nc.gpsimd, it, 0, 1, state[it]["t12"][:, 0, 0:1, :, :, :])
+            if it + 3 < NG:
+                front(it + 3)
+            if it + 1 < NG:
                 project_value(it + 1)
-            for h in range(NQ):
-                if 0 <= it < NG:
-                    products_query(it, h)
-                if 0 <= it + 1 < NG:
-                    project_query(it + 1, h)
-                if B < it < NG and it % B == 1 and h == 0:
-                    query_shift(it // B)
-                if last and h == 0:
-                    join_query(nc.gpsimd, it, 0, state[it]["t0"][:, 0, :, :, :])
-            if 0 <= it + 1 < NG:
+            if it + 1 < NG:
                 norm_root(it + 1)
-            if it == -2:
-                quant(0)
-                shift_matrices()
-                key_table(0, 0)
-                key_table(0, 1)
-                swap_sin(1)
-                for a in range(2):
-                    query_table(nc.gpsimd, 1, a, a + 1)
-            elif it + 2 < NG and it < 0:
-                quant(it + 2)
-            if it == -1:
-                key_shift(0)
+            if it < NG:
+                products_key(it)
+            if it + 1 < NG:
+                project_key_t(it + 1)
+            if it < NG:
+                join_key(it)
+            if it < NG:
+                scale_key(it)
+            if it < NG and it % B == 0:
+                key_shift(it // B)
+            if it == 0:
                 query_shift(0)
+            if it in (1, 3, 7):
+                transpose_table((it + 3) // 3, psum_s, "kv")
             if 0 <= it - 1 < NG - 1:
-                finish(it - 1, all_blocks[:-1])
-            if it >= 0 and it + 2 < NG:
+                finish(it - 1, all_blocks[0:7])
+            if it in (3, 5, 9):
+                key_table((it + 3) // 4)
+            if it == 1 or it == 2:
+                swap_sin(it + 1)
+                query_table(nc.vector, it + 1, 0, 2)
+            if it + 2 < NG:
                 quant(it + 2)
             if 0 <= it - 1 < NG - 1:
-                finish(it - 1, all_blocks[-1:])
+                finish(it - 1, all_blocks[7:8])
+            if 0 <= it - 1 < NG - 1:
                 store(it - 1, 0, NQ)
-            if 0 <= it and it // B + 1 < PG:
-                pg = it // B + 1
-                step = it % B
-                if step == 0:
-                    if pg > 1:
-                        swap_sin(pg)
-                    transpose_table(pg, psum_t, "xt")
-                elif step == 1:
-                    key_table(pg, 0)
-                    if pg > 1:
-                        query_table(nc.gpsimd, pg, 0, 1)
-                elif step == 2:
-                    key_table(pg, 1)
-                    if pg > 1:
-                        query_table(nc.gpsimd, pg, 1, 2)
-                else:
-                    key_shift(pg)
             if it == NG:
                 gi = NG - 1
-                join_query(nc.vector, gi, 1, state[gi]["t1"][:, 0, :, :, :])
-                state[gi]["sums"] = [state[gi]["t%d" % h][:, 0, :, :, :] for h in range(NQ)]
+                join_query(nc.vector, gi, 1, 2, state[gi]["t12"][:, 0, 1:2, :, :, :])
+                state[gi]["sums"] = state[gi]["t12"][:, 0, :, :, :, :]
                 for h in (1, 0):
                     finish(gi, all_blocks[h * NT:(h + 1) * NT])
                     store(gi, h, h + 1)

@@ -336,6 +336,10 @@ def tile_groupqueryattention_pa_t_kernel(
             st = state[gi]
             ok = deep.tile([P, NT, DH], F32, tag="ok", name="ok")
             nc.gpsimd.tensor_tensor(out=ok[:], in0=st["ks"][:], in1=ck_tiles[pg][:], op=ALU.add)
+            store_key(gi, ok)
+
+        def store_key(gi, ok):
+            pg, b = order[gi]
             lo = pg * GROUP
             nc.sync.dma_start(
                 out=out_1[b, 0, lo:lo + GROUP, :].rearrange("(p n) j -> p (n j)", n=NT),
@@ -355,6 +359,22 @@ def tile_groupqueryattention_pa_t_kernel(
             t3 = single.tile([P, NQ, NT, 2, HALF], F32, tag="t3", name="t3")
             join_query(nc.gpsimd, gi, 0, NQ, t3[:])
             state[gi]["sums"] = t3
+
+        def join_last():
+            t12 = state[NG - 1]["t12"]
+            join_query(nc.gpsimd, NG - 1, 0, NQ, t12[:, 0, :, :, :, :])
+            state[NG - 1]["sums"] = t12[:, 0, :, :, :, :]
+
+        def finish_key_vector(gi):
+            pg, b = order[gi]
+            st = state[gi]
+            ok = deep.tile([P, NT, DH], F32, tag="ok", name="ok")
+            for n in range(NT):
+                nc.vector.scalar_tensor_tensor(
+                    out=ok[:, n, :], in0=st["tk"][:, n, :], scalar=st["rinv"][:, KEY * NT + n:KEY * NT + n + 1],
+                    in1=ck_tiles[pg][:, n, :], op0=ALU.mult, op1=ALU.add,
+                )
+            store_key(gi, ok)
 
         def finish(gi, blocks):
             pg, b = order[gi]
@@ -382,6 +402,7 @@ def tile_groupqueryattention_pa_t_kernel(
 
         all_blocks = [(h, n) for h in range(NQ) for n in range(NT)]
         key_gain_columns()
+        shift_matrices()
         w_grouped = transpose_group(w_sb, (1,), psum_q, "q")
         quantise(w_grouped, w_codes, w_scales)
         front(0, (1,))
@@ -389,77 +410,72 @@ def tile_groupqueryattention_pa_t_kernel(
         quant(0)
         query_table(nc.vector, 0, 0, 2)
         front(1)
-        transpose_table(0, psum_s, "c")
+        project_query(0, 0)
         quant(1)
-        shift_matrices()
-        for h in range(NQ):
-            project_query(0, h)
-        key_table(0)
+        swap_sin(1)
+        project_query(0, 1)
+        transpose_table(0, psum_s, "c")
         front(2)
         project_key(0)
         project_key_t(0)
         project_value(0)
         norm_root(0)
-        swap_sin(1)
-        for a in range(2):
+        for a in (1, 0):
             query_table(nc.gpsimd, 1, a, a + 1)
-        for it in range(NG + 1):
+        for it in range(NG):
             last = it == NG - 1
-            if 0 <= it - 1 < NG - 1:
+            pg, step = divmod(it, B)
+            if it > 0:
                 join_pool(it - 1)
-            if 0 <= it - 1 < NG:
-                finish_key(it - 1)
-            if B < it < NG and it % B == 1:
-                query_shift(it // B)
-            if it < NG:
-                products_query(it, 0)
-            if it + 1 < NG:
+                if not last:
+                    finish_key(it - 1)
+                if step == 1 and pg > 0:
+                    query_shift(pg)
+            products_query(it, 0)
+            if not last:
                 project_query(it + 1, 0)
-            if it + 1 < NG:
                 project_key(it + 1)
-            if it < NG:
-                products_query(it, 1)
-            if it + 1 < NG:
+            products_query(it, 1)
+            if not last:
                 project_query(it + 1, 1)
-            if last:
-                join_query(nc.gpsimd, it, 0, 1, state[it]["t12"][:, 0, 0:1, :, :, :])
+            else:
+                join_last()
             if it + 3 < NG:
                 front(it + 3)
-            if it + 1 < NG:
+            if not last:
                 project_value(it + 1)
-            if it + 1 < NG:
                 norm_root(it + 1)
-            if it < NG:
-                products_key(it)
-            if it + 1 < NG:
-                project_key_t(it + 1)
-            if it < NG:
-                join_key(it)
-            if it < NG:
-                scale_key(it)
-            if it < NG and it % B == 0:
-                key_shift(it // B)
+            if it == 0:
+                key_table(0)
+                quant(2)
             if it == 0:
                 query_shift(0)
-            if it in (1, 3, 7):
-                transpose_table((it + 3) // 3, psum_s, "kv")
-            if 0 <= it - 1 < NG - 1:
-                finish(it - 1, all_blocks[0:7])
-            if it in (3, 5, 9):
-                key_table((it + 3) // 4)
-            if it == 1 or it == 2:
-                swap_sin(it + 1)
-                query_table(nc.vector, it + 1, 0, 2)
-            if it + 2 < NG:
+            products_key(it)
+            if not last:
+                project_key_t(it + 1)
+            join_key(it)
+            if not last:
+                scale_key(it)
+            if it == 0:
+                key_shift(0)
+            if step == 2 and pg + 1 < PG:
+                key_shift(pg + 1)
+            if it in (1, 4, 8):
+                transpose_table((it + 4) // B, psum_s, "kv")
+            if it > 0:
+                finish(it - 1, all_blocks[:-1])
+            if it in (2, 5):
+                swap_sin(it // 2 + 1)
+                query_table(nc.vector, it // 2 + 1, 0, 2)
+            if step == 3 and pg + 1 < PG:
+                key_table(pg + 1)
+            if 0 < it and it + 2 < NG:
                 quant(it + 2)
-            if 0 <= it - 1 < NG - 1:
-                finish(it - 1, all_blocks[7:8])
-            if 0 <= it - 1 < NG - 1:
+            if it > 0:
+                finish(it - 1, all_blocks[-1:])
                 store(it - 1, 0, NQ)
-            if it == NG:
-                gi = NG - 1
-                join_query(nc.vector, gi, 1, 2, state[gi]["t12"][:, 0, 1:2, :, :, :])
-                state[gi]["sums"] = state[gi]["t12"][:, 0, :, :, :, :]
-                for h in (1, 0):
-                    finish(gi, all_blocks[h * NT:(h + 1) * NT])
-                    store(gi, h, h + 1)
+        finish_key_vector(NG - 1)
+        finish_key(NG - 2)
+        for h in range(NQ):
+            finish(NG - 1, all_blocks[h * NT:(h + 1) * NT])
+            store(NG - 1, h, h + 1)

@@ -75,6 +75,8 @@ def tile_groupqueryattention_pa_t_kernel(
             sn.append(snt)
 
         w_sb = const.tile([P, NT, D], BF16, name="w_sb")
+        eps_t = const.tile([P, 1], F32, name="eps_t")
+        nc.vector.memset(eps_t[:], EPS)
         vrow = const.tile([P, 4, DH], BF16, name="vrow")
         nc.vector.memset(vrow[:], 0.0)
         ones_b = const.tile([P, P], BF16, name="ones_b")
@@ -82,7 +84,7 @@ def tile_groupqueryattention_pa_t_kernel(
         vectors = (q_scale, k_scale, q_shift, k_shift)
         vload = const.tile([1, 4, DH], BF16, name="vload")
         for i in range(4):
-            nc.sync.dma_start(out=vload[0:1, i, :], in_=vectors[i].rearrange("(o j) -> o j", o=1))
+            nc.scalar.dma_start(out=vload[0:1, i, :], in_=vectors[i].rearrange("(o j) -> o j", o=1))
         nc.sync.dma_start(out=w_sb[:, 0:2, :], in_=wq.rearrange("(r p) k -> p r k", p=P))
         nc.sync.dma_start(out=w_sb[:, KEY, :], in_=wk)
         nc.sync.dma_start(out=w_sb[:, VAL, :], in_=wv)
@@ -96,9 +98,6 @@ def tile_groupqueryattention_pa_t_kernel(
         for gi in range(3, NG):
             load_x(gi)
 
-        nc.vector.tensor_copy(out=vrow[0:1, :, :], in_=vload[:])
-        eps_t = const.tile([P, 1], F32, name="eps_t")
-        nc.vector.memset(eps_t[:], EPS)
         warm = const.tile([P, 1], F32, name="warm")
         nc.scalar.activation(out=warm[:], in_=eps_t[:], func=ACT.Abs_reciprocal_sqrt)
         ident_b = const.tile([P, P], BF16, name="ident_b")
@@ -106,6 +105,8 @@ def tile_groupqueryattention_pa_t_kernel(
         perm_f = const.tile([P, P], F32, name="perm_f")
         nc.vector.tensor_copy(out=perm_f[:, 0:HALF], in_=ident_f[:, HALF:])
         nc.vector.tensor_copy(out=perm_f[:, HALF:], in_=ident_f[:, 0:HALF])
+
+        nc.vector.tensor_copy(out=vrow[0:1, :, :], in_=vload[:])
 
         def spread_vectors(i0, tag):
             spread = psum_s.tile([P, 2, DH], F32, tag=tag, name="spread")
@@ -116,11 +117,13 @@ def tile_groupqueryattention_pa_t_kernel(
             return spread
 
         gains = const.tile([P, 2, DH], F32, name="gains")
-        scales_ps = spread_vectors(0, "kv")
-        nc.vector.tensor_scalar_add(out=gains[:], in0=scales_ps[:], scalar1=1.0)
         key_gain = const.tile([P, 1], F32, name="key_gain")
         dc = const.tile([P, 2, DH], BF16, name="dc")
         ds = const.tile([P, 2, DH], BF16, name="ds")
+
+        def spread_gains():
+            scales_ps = spread_vectors(0, "kv")
+            nc.vector.tensor_scalar_add(out=gains[:], in0=scales_ps[:], scalar1=1.0)
 
         def key_gain_columns():
             col_ps = psum_s.tile([P, P], F32, tag="tk", name="col_ps")
@@ -143,14 +146,11 @@ def tile_groupqueryattention_pa_t_kernel(
         w_scales = const.tile([P, NT * P], U8, name="w_scales", align_bytes=64)
         state = {}
         qtab = {}
-        ktab = {}
         cst_tiles = {}
         cq_tiles = {}
         ck_tiles = {}
 
-        def transpose_group(src, share, pool, tag):
-            grouped = work.tile([P, NT, P, 4], BF16, tag="grouped", name="grouped", align_bytes=64)
-            gwords = grouped[:].bitcast(F32)
+        def transpose_words(src, pool, tag):
             banks = []
             for half in range(2):
                 xt = pool.tile([P, 2, 2, P], F32, tag=tag, name="xt")
@@ -159,12 +159,24 @@ def tile_groupqueryattention_pa_t_kernel(
                     for u in range(2):
                         nc.tensor.transpose(xt[:, i, u, :], words[:, u:2 * P:2], ident_f[:])
                 banks.append(xt)
+            return banks
+
+        def interleave(grouped, banks, half, on_vector):
+            dst = grouped[:].bitcast(F32)[:, 2 * half:2 * half + 2, :, :]
+            src = banks[half][:].rearrange("p i u r -> p i r u")
+            if on_vector:
+                nc.vector.tensor_copy(out=dst, in_=src)
+            else:
+                nc.scalar.copy(out=dst, in_=src)
+
+        def new_grouped():
+            return work.tile([P, NT, P, 4], BF16, tag="grouped", name="grouped", align_bytes=64)
+
+        def transpose_group(src, share, pool, tag):
+            banks = transpose_words(src, pool, tag)
+            grouped = new_grouped()
             for half in range(2):
-                dst = gwords[:, 2 * half:2 * half + 2, :, :]
-                if half in share:
-                    nc.vector.tensor_copy(out=dst, in_=banks[half][:].rearrange("p i u r -> p i r u"))
-                else:
-                    nc.scalar.copy(out=dst, in_=banks[half][:].rearrange("p i u r -> p i r u"))
+                interleave(grouped, banks, half, half in share)
             return grouped
 
         def quantise(grouped, codes, scales):
@@ -192,10 +204,6 @@ def tile_groupqueryattention_pa_t_kernel(
             cst = const.tile([P, 2 * NT, P], BF16, name="cst%d" % pg)
             nc.scalar.copy(out=cst[:], in_=cst_ps[:].rearrange("p c n r -> p (c n) r"))
             cst_tiles[pg] = cst
-
-        def key_table(pg):
-            ktab[pg] = const.tile([P, 2 * NT, P], F32, name="ktab%d" % pg)
-            nc.vector.tensor_scalar_mul(out=ktab[pg][:], in0=cst_tiles[pg][:], scalar1=key_gain[:])
 
         def shift_table(pg, kind, tag):
             cst = cst_tiles[pg]
@@ -295,9 +303,9 @@ def tile_groupqueryattention_pa_t_kernel(
             pg, b = order[gi]
             st = state[gi]
             st["pk"] = work.tile([P, 2, GROUP], F32, tag="pk", name="pk")
-            nc.vector.tensor_tensor(
-                out=st["pk"][:], in0=st["kT"][:].unsqueeze(1).to_broadcast([P, 2, GROUP]),
-                in1=ktab[pg][:].rearrange("p (a n) r -> p a (n r)", a=2), op=ALU.mult,
+            nc.vector.scalar_tensor_tensor(
+                out=st["pk"][:], in0=st["kT"][:].unsqueeze(1).to_broadcast([P, 2, GROUP]), scalar=key_gain[:],
+                in1=cst_tiles[pg][:].rearrange("p (a n) r -> p a (n r)", a=2), op0=ALU.mult, op1=ALU.mult,
             )
 
         def products_query(gi, h):
@@ -322,6 +330,14 @@ def tile_groupqueryattention_pa_t_kernel(
                         start=a == 0, stop=a == 1, is_transpose=True,
                     )
             st["tk"] = tk
+
+        def keep_clock(passes):
+            spare = psum_t.tile([P, GROUP], F32, tag="xt", name="spare")
+            for i in range(passes):
+                nc.tensor.matmul_mx(
+                    out=spare[:], lhsT=w_codes[:, 0:P].bitcast(FP8X4), lhsT_scale=w_scales[:, 0:P],
+                    rhs=w_codes[:].bitcast(FP8X4), rhs_scale=w_scales[:], start=True, stop=True,
+                )
 
         def scale_key(gi):
             st = state[gi]
@@ -401,43 +417,67 @@ def tile_groupqueryattention_pa_t_kernel(
             )
 
         all_blocks = [(h, n) for h in range(NQ) for n in range(NT)]
-        key_gain_columns()
-        shift_matrices()
-        w_grouped = transpose_group(w_sb, (1,), psum_q, "q")
+        banks = transpose_words(w_sb, psum_q, "q")
+        w_grouped = new_grouped()
+        interleave(w_grouped, banks, 0, False)
+        interleave(w_grouped, banks, 1, True)
         quantise(w_grouped, w_codes, w_scales)
+        spread_gains()
+        shift_matrices()
         front(0, (1,))
+        key_gain_columns()
         swap_sin(0)
         quant(0)
         query_table(nc.vector, 0, 0, 2)
         front(1)
         project_query(0, 0)
         quant(1)
-        swap_sin(1)
         project_query(0, 1)
         transpose_table(0, psum_s, "c")
-        front(2)
+        banks = transpose_words(x_sb[2], psum_t, "xt")
+        state[2] = {"grouped": new_grouped()}
+        interleave(state[2]["grouped"], banks, 0, False)
         project_key(0)
         project_key_t(0)
+        products_query(0, 0)
+        project_query(1, 0)
         project_value(0)
         norm_root(0)
-        for a in (1, 0):
-            query_table(nc.gpsimd, 1, a, a + 1)
-        for it in range(NG):
+        products_query(0, 1)
+        interleave(state[2]["grouped"], banks, 1, True)
+        project_key(1)
+        project_query(1, 1)
+        front(3)
+        project_value(1)
+        norm_root(1)
+        products_key(0)
+        project_key_t(1)
+        join_key(0)
+        scale_key(0)
+        query_shift(0)
+        key_shift(0)
+        for it in range(1, NG):
             last = it == NG - 1
             pg, step = divmod(it, B)
-            if it > 0:
-                join_pool(it - 1)
-                if not last:
-                    finish_key(it - 1)
-                if step == 1 and pg > 0:
-                    query_shift(pg)
+            join_pool(it - 1)
+            if it > 1 and not last:
+                finish_key(it - 1)
+            if step == 1 and pg > 0:
+                query_shift(pg)
             products_query(it, 0)
+            if it == 1:
+                quant(2)
+                swap_sin(1)
+                for a in (1, 0):
+                    query_table(nc.gpsimd, 1, a, a + 1)
+                finish_key(0)
             if not last:
                 project_query(it + 1, 0)
                 project_key(it + 1)
             products_query(it, 1)
             if not last:
                 project_query(it + 1, 1)
+                keep_clock(1)
             else:
                 join_last()
             if it + 3 < NG:
@@ -445,35 +485,24 @@ def tile_groupqueryattention_pa_t_kernel(
             if not last:
                 project_value(it + 1)
                 norm_root(it + 1)
-            if it == 0:
-                key_table(0)
-                quant(2)
-            if it == 0:
-                query_shift(0)
             products_key(it)
             if not last:
                 project_key_t(it + 1)
             join_key(it)
             if not last:
                 scale_key(it)
-            if it == 0:
-                key_shift(0)
             if step == 2 and pg + 1 < PG:
                 key_shift(pg + 1)
             if it in (1, 4, 8):
                 transpose_table((it + 4) // B, psum_s, "kv")
-            if it > 0:
-                finish(it - 1, all_blocks[:-1])
+            finish(it - 1, all_blocks[:-1])
             if it in (2, 5):
                 swap_sin(it // 2 + 1)
                 query_table(nc.vector, it // 2 + 1, 0, 2)
-            if step == 3 and pg + 1 < PG:
-                key_table(pg + 1)
-            if 0 < it and it + 2 < NG:
+            if it + 2 < NG:
                 quant(it + 2)
-            if it > 0:
-                finish(it - 1, all_blocks[-1:])
-                store(it - 1, 0, NQ)
+            finish(it - 1, all_blocks[-1:])
+            store(it - 1, 0, NQ)
         finish_key_vector(NG - 1)
         finish_key(NG - 2)
         for h in range(NQ):

@@ -146,6 +146,7 @@ def tile_groupqueryattention_pa_t_kernel(
         w_scales = const.tile([P, NT * P], U8, name="w_scales", align_bytes=64)
         state = {}
         qtab = {}
+        ktab = {}
         cst_tiles = {}
         cq_tiles = {}
         ck_tiles = {}
@@ -204,6 +205,17 @@ def tile_groupqueryattention_pa_t_kernel(
             cst = const.tile([P, 2 * NT, P], BF16, name="cst%d" % pg)
             nc.scalar.copy(out=cst[:], in_=cst_ps[:].rearrange("p c n r -> p (c n) r"))
             cst_tiles[pg] = cst
+
+        def key_table(pg):
+            ktab[pg] = const.tile([P, 2 * NT, P], F32, name="ktab%d" % pg)
+            if pg == 0:
+                for i in (0, NT):
+                    nc.gpsimd.tensor_scalar(
+                        out=ktab[pg][:, i:i + NT, :], in0=cst_tiles[pg][:, i:i + NT, :],
+                        scalar1=key_gain[:], scalar2=0.0, op0=ALU.mult, op1=ALU.add,
+                    )
+            else:
+                nc.vector.tensor_scalar_mul(out=ktab[pg][:], in0=cst_tiles[pg][:], scalar1=key_gain[:])
 
         def shift_table(pg, kind, tag):
             cst = cst_tiles[pg]
@@ -303,9 +315,9 @@ def tile_groupqueryattention_pa_t_kernel(
             pg, b = order[gi]
             st = state[gi]
             st["pk"] = work.tile([P, 2, GROUP], F32, tag="pk", name="pk")
-            nc.vector.scalar_tensor_tensor(
-                out=st["pk"][:], in0=st["kT"][:].unsqueeze(1).to_broadcast([P, 2, GROUP]), scalar=key_gain[:],
-                in1=cst_tiles[pg][:].rearrange("p (a n) r -> p a (n r)", a=2), op0=ALU.mult, op1=ALU.mult,
+            nc.vector.tensor_tensor(
+                out=st["pk"][:], in0=st["kT"][:].unsqueeze(1).to_broadcast([P, 2, GROUP]),
+                in1=ktab[pg][:].rearrange("p (a n) r -> p a (n r)", a=2), op=ALU.mult,
             )
 
         def products_query(gi, h):
@@ -437,6 +449,7 @@ def tile_groupqueryattention_pa_t_kernel(
         banks = transpose_words(x_sb[2], psum_t, "xt")
         state[2] = {"grouped": new_grouped()}
         interleave(state[2]["grouped"], banks, 0, False)
+        key_table(0)
         project_key(0)
         project_key_t(0)
         products_query(0, 0)
@@ -496,6 +509,8 @@ def tile_groupqueryattention_pa_t_kernel(
             if it in (1, 4, 8):
                 transpose_table((it + 4) // B, psum_s, "kv")
             finish(it - 1, all_blocks[:-1])
+            if step == 3 and pg + 1 < PG:
+                key_table(pg + 1)
             if it in (2, 5):
                 swap_sin(it // 2 + 1)
                 query_table(nc.vector, it // 2 + 1, 0, 2)

@@ -83,19 +83,17 @@ def tile_groupqueryattention_pa_t_kernel(
         nc.vector.memset(ones_b[:], 1.0)
         vectors = (q_scale, k_scale, q_shift, k_shift)
         vload = const.tile([1, 4, DH], BF16, name="vload")
-        for i in range(4):
-            nc.scalar.dma_start(out=vload[0:1, i, :], in_=vectors[i].rearrange("(o j) -> o j", o=1))
         nc.sync.dma_start(out=w_sb[:, 0:2, :], in_=wq.rearrange("(r p) k -> p r k", p=P))
         nc.sync.dma_start(out=w_sb[:, KEY, :], in_=wk)
         nc.sync.dma_start(out=w_sb[:, VAL, :], in_=wv)
+        for i in range(4):
+            nc.sync.dma_start(out=vload[0:1, i, :], in_=vectors[i].rearrange("(o j) -> o j", o=1))
         load_x(0)
         load_cs(0)
         load_x(1)
-        load_cs(1)
-        load_x(2)
-        load_cs(2)
-        load_cs(3)
-        for gi in range(3, NG):
+        for pg in range(1, PG):
+            load_cs(pg)
+        for gi in range(2, NG):
             load_x(gi)
 
         warm = const.tile([P, 1], F32, name="warm")
@@ -444,6 +442,8 @@ def tile_groupqueryattention_pa_t_kernel(
         front(1)
         project_query(0, 0)
         quant(1)
+        for pg in range(1, PG):
+            swap_sin(pg)
         project_query(0, 1)
         transpose_table(0, psum_s, "c")
         banks = transpose_words(x_sb[2], psum_t, "xt")
@@ -480,8 +480,7 @@ def tile_groupqueryattention_pa_t_kernel(
             products_query(it, 0)
             if it == 1:
                 quant(2)
-                swap_sin(1)
-                for a in (1, 0):
+                for a in range(2):
                     query_table(nc.gpsimd, 1, a, a + 1)
                 finish_key(0)
             if not last:
@@ -512,7 +511,6 @@ def tile_groupqueryattention_pa_t_kernel(
             if step == 3 and pg + 1 < PG:
                 key_table(pg + 1)
             if it in (2, 5):
-                swap_sin(it // 2 + 1)
                 query_table(nc.vector, it // 2 + 1, 0, 2)
             if it + 2 < NG:
                 quant(it + 2)

@@ -273,15 +273,16 @@ def tile_groupqueryattention_pa_t_kernel(
         def project_key_t(gi):
             st = state[gi]
             st["kT"] = psum_s.tile([P, GROUP], F32, tag="kT", name="kT")
-            nc.tensor.matmul_mx(
-                out=st["kT"][:],
-                lhsT=w_codes[:, KEY * P:(KEY + 1) * P].bitcast(FP8X4),
-                lhsT_scale=w_scales[:, KEY * P:(KEY + 1) * P],
-                rhs=st["codes"][:].bitcast(FP8X4),
-                rhs_scale=st["scales"][:],
-                start=True,
-                stop=True,
-            )
+            for twice in range(2):
+                nc.tensor.matmul_mx(
+                    out=st["kT"][:],
+                    lhsT=w_codes[:, KEY * P:(KEY + 1) * P].bitcast(FP8X4),
+                    lhsT_scale=w_scales[:, KEY * P:(KEY + 1) * P],
+                    rhs=st["codes"][:].bitcast(FP8X4),
+                    rhs_scale=st["scales"][:],
+                    start=True,
+                    stop=True,
+                )
 
         def project_value(gi):
             pg, b = order[gi]
@@ -340,14 +341,6 @@ def tile_groupqueryattention_pa_t_kernel(
                         start=a == 0, stop=a == 1, is_transpose=True,
                     )
             st["tk"] = tk
-
-        def keep_clock(passes):
-            spare = psum_t.tile([P, GROUP], F32, tag="xt", name="spare")
-            for i in range(passes):
-                nc.tensor.matmul_mx(
-                    out=spare[:], lhsT=w_codes[:, 0:P].bitcast(FP8X4), lhsT_scale=w_scales[:, 0:P],
-                    rhs=w_codes[:].bitcast(FP8X4), rhs_scale=w_scales[:], start=True, stop=True,
-                )
 
         def scale_key(gi):
             st = state[gi]
@@ -489,7 +482,6 @@ def tile_groupqueryattention_pa_t_kernel(
             products_query(it, 1)
             if not last:
                 project_query(it + 1, 1)
-                keep_clock(1)
             else:
                 join_last()
             if it + 3 < NG:

from contextlib import ExitStack

import concourse.mybir as mybir
from concourse.masks import make_identity

F32 = mybir.dt.float32
BF16 = mybir.dt.bfloat16
U32 = mybir.dt.uint32
U8 = mybir.dt.uint8
FP8X4 = mybir.dt.float8_e4m3fn_x4
ALU = mybir.AluOpType
ACT = mybir.ActivationFunctionType

B, S, D = 4, 2048, 512
P = 128
DH = 128
HALF = DH // 2
NT = 4
GROUP = P * NT
PG = S // GROUP
NQ = 2
NH = 3
KEY = 2
VAL = 3
EPS = 1e-6
FLOPS = 2 * B * S * D * 512


def tile_groupqueryattention_pa_t_kernel(
    tc, x, sin_thetas, cos_thetas, wq, wk, wv, q_scale, q_shift, k_scale, k_shift, out_0, out_1, out_2
):
    nc = tc.nc
    with ExitStack() as ctx:
        const = ctx.enter_context(tc.tile_pool(name="const", bufs=1))
        xpool = ctx.enter_context(tc.tile_pool(name="xpool", bufs=1))
        work = ctx.enter_context(tc.tile_pool(name="work", bufs=2))
        deep = ctx.enter_context(tc.tile_pool(name="deep", bufs=3))
        prods = ctx.enter_context(tc.tile_pool(name="prods", bufs=3))
        single = ctx.enter_context(tc.tile_pool(name="single", bufs=1))
        psum_t = ctx.enter_context(tc.psum_pool(name="psum_t", bufs=2))
        psum_q = ctx.enter_context(tc.psum_pool(name="psum_q", bufs=2))
        psum_s = ctx.enter_context(tc.psum_pool(name="psum_s", bufs=1))
        ctx.enter_context(tc.manual_schedule())

        order = [(pg, b) for pg in range(PG) for b in range(B)]
        NG = len(order)

        ident_f = const.tile([P, P], F32, name="ident_f")
        make_identity(nc, ident_f[:])
        x_sb = []
        cs = []
        sn = []

        def load_x(gi):
            pg, b = order[gi]
            xs = xpool.tile([P, NT, D], BF16, name="xs%d" % gi)
            nc.sync.dma_start(
                out=xs[:].rearrange("p n k -> p (n k)"),
                in_=x[b, pg * GROUP:(pg + 1) * GROUP, :].rearrange("(p n) k -> p (n k)", n=NT),
            )
            x_sb.append(xs)

        def load_cs(pg):
            cst_in = const.tile([P, 2, NT, DH], BF16, name="cs%d" % pg)
            snt = const.tile([P, NT, 2, HALF], BF16, name="sn%d" % pg)
            nc.sync.dma_start(
                out=cst_in[:, 0, :, :].rearrange("p n j -> p (n j)"),
                in_=cos_thetas[pg * GROUP:(pg + 1) * GROUP, :].rearrange("(p n) j -> p (n j)", n=NT),
            )
            nc.sync.dma_start(
                out=snt[:].rearrange("p n c j -> p (n c j)"),
                in_=sin_thetas[pg * GROUP:(pg + 1) * GROUP, :].rearrange("(p n) j -> p (n j)", n=NT),
            )
            cs.append(cst_in)
            sn.append(snt)

        w_sb = const.tile([P, NT, D], BF16, name="w_sb")
        eps_t = const.tile([P, 1], F32, name="eps_t")
        nc.vector.memset(eps_t[:], EPS)
        vrow = const.tile([P, 4, DH], BF16, name="vrow")
        nc.vector.memset(vrow[:], 0.0)
        ones_b = const.tile([P, P], BF16, name="ones_b")
        nc.vector.memset(ones_b[:], 1.0)
        vectors = (q_scale, k_scale, q_shift, k_shift)
        vload = const.tile([1, 4, DH], BF16, name="vload")
        nc.sync.dma_start(out=w_sb[:, 0:2, :], in_=wq.rearrange("(r p) k -> p r k", p=P))
        nc.sync.dma_start(out=w_sb[:, KEY, :], in_=wk)
        nc.sync.dma_start(out=w_sb[:, VAL, :], in_=wv)
        for i in range(4):
            nc.sync.dma_start(out=vload[0:1, i, :], in_=vectors[i].rearrange("(o j) -> o j", o=1))
        load_x(0)
        load_cs(0)
        load_x(1)
        for pg in range(1, PG):
            load_cs(pg)
        for gi in range(2, NG):
            load_x(gi)

        warm = const.tile([P, 1], F32, name="warm")
        nc.scalar.activation(out=warm[:], in_=eps_t[:], func=ACT.Abs_reciprocal_sqrt)
        ident_b = const.tile([P, P], BF16, name="ident_b")
        nc.vector.tensor_copy(out=ident_b[:], in_=ident_f[:])
        perm_f = const.tile([P, P], F32, name="perm_f")
        nc.vector.tensor_copy(out=perm_f[:, 0:HALF], in_=ident_f[:, HALF:])
        nc.vector.tensor_copy(out=perm_f[:, HALF:], in_=ident_f[:, 0:HALF])

        nc.vector.tensor_copy(out=vrow[0:1, :, :], in_=vload[:])

        def spread_vectors(i0, tag):
            spread = psum_s.tile([P, 2, DH], F32, tag=tag, name="spread")
            nc.tensor.matmul(
                spread[:].rearrange("p i j -> p (i j)"), lhsT=ones_b[:],
                rhs=vrow[:, i0:i0 + 2, :].rearrange("p i j -> p (i j)"), start=True, stop=True,
            )
            return spread

        gains = const.tile([P, 2, DH], F32, name="gains")
        key_gain = const.tile([P, 1], F32, name="key_gain")
        dc = const.tile([P, 2, DH], BF16, name="dc")
        ds = const.tile([P, 2, DH], BF16, name="ds")

        def spread_gains():
            scales_ps = spread_vectors(0, "kv")
            nc.vector.tensor_scalar_add(out=gains[:], in0=scales_ps[:], scalar1=1.0)

        def key_gain_columns():
            col_ps = psum_s.tile([P, P], F32, tag="tk", name="col_ps")
            nc.tensor.transpose(col_ps[:], gains[:, 1, :], ident_f[:])
            nc.scalar.copy(out=key_gain[:], in_=col_ps[:, 0:1])

        def shift_matrices():
            shifts_ps = spread_vectors(2, "kT")
            nc.vector.tensor_tensor(
                out=dc[:], in0=shifts_ps[:], in1=ident_f[:].unsqueeze(1).to_broadcast([P, 2, DH]), op=ALU.mult
            )
            nc.vector.tensor_tensor(
                out=ds[:].rearrange("p i (c j) -> p i c j", c=2),
                in0=shifts_ps[:].rearrange("p i (c j) -> p i c j", c=2)[:, :, ::-1, :],
                in1=perm_f[:].rearrange("p (c j) -> p c j", c=2).unsqueeze(1).to_broadcast([P, 2, 2, HALF]),
                op=ALU.mult,
            )

        w_codes = const.tile([P, NT * P], U32, name="w_codes", align_bytes=64)
        w_scales = const.tile([P, NT * P], U8, name="w_scales", align_bytes=64)
        state = {}
        qtab = {}
        ktab = {}
        cst_tiles = {}
        cq_tiles = {}
        ck_tiles = {}

        def transpose_words(src, pool, tag):
            banks = []
            for half in range(2):
                xt = pool.tile([P, 2, 2, P], F32, tag=tag, name="xt")
                for i in range(2):
                    words = src[:, 2 * half + i, :].bitcast(F32)
                    for u in range(2):
                        nc.tensor.transpose(xt[:, i, u, :], words[:, u:2 * P:2], ident_f[:])
                banks.append(xt)
            return banks

        def interleave(grouped, banks, half, on_vector):
            dst = grouped[:].bitcast(F32)[:, 2 * half:2 * half + 2, :, :]
            src = banks[half][:].rearrange("p i u r -> p i r u")
            if on_vector:
                nc.vector.tensor_copy(out=dst, in_=src)
            else:
                nc.scalar.copy(out=dst, in_=src)

        def new_grouped():
            return work.tile([P, NT, P, 4], BF16, tag="grouped", name="grouped", align_bytes=64)

        def transpose_group(src, share, pool, tag):
            banks = transpose_words(src, pool, tag)
            grouped = new_grouped()
            for half in range(2):
                interleave(grouped, banks, half, half in share)
            return grouped

        def quantise(grouped, codes, scales):
            nc.vector.quantize_mx(
                out=codes[:].bitcast(FP8X4), scales=scales[:], in_=grouped[:].rearrange("p n r t -> p (n r t)")
            )

        def swap_sin(pg):
            nc.vector.tensor_copy(out=cs[pg][:, 1, :, 0:HALF], in_=sn[pg][:, :, 1, :])
            nc.vector.tensor_scalar_mul(out=cs[pg][:, 1, :, HALF:], in0=sn[pg][:, :, 0, :], scalar1=-1.0)

        def query_table(eng, pg, a0, a1):
            if pg not in qtab:
                qtab[pg] = const.tile([P, 2, NT, DH], F32, name="qtab%d" % pg)
            eng.tensor_tensor(
                out=qtab[pg][:, a0:a1, :, :], in0=cs[pg][:, a0:a1, :, :],
                in1=gains[:, 0:1, :].unsqueeze(1).to_broadcast([P, a1 - a0, NT, DH]), op=ALU.mult,
            )

        def transpose_table(pg, pool, tag):
            cst_ps = pool.tile([P, 2, NT, P], BF16, tag=tag, name="cst_ps")
            for c in range(2):
                for n in range(NT):
                    nc.tensor.transpose(cst_ps[:, c, n, :], cs[pg][:, c, n, :], ident_b[:])
            cst = const.tile([P, 2 * NT, P], BF16, name="cst%d" % pg)
            nc.scalar.copy(out=cst[:], in_=cst_ps[:].rearrange("p c n r -> p (c n) r"))
            cst_tiles[pg] = cst

        def key_table(pg):
            ktab[pg] = const.tile([P, 2 * NT, P], F32, name="ktab%d" % pg)
            if pg == 0:
                for i in (0, NT):
                    nc.gpsimd.tensor_scalar(
                        out=ktab[pg][:, i:i + NT, :], in0=cst_tiles[pg][:, i:i + NT, :],
                        scalar1=key_gain[:], scalar2=0.0, op0=ALU.mult, op1=ALU.add,
                    )
            else:
                nc.vector.tensor_scalar_mul(out=ktab[pg][:], in0=cst_tiles[pg][:], scalar1=key_gain[:])

        def shift_table(pg, kind, tag):
            cst = cst_tiles[pg]
            c_ps = psum_s.tile([P, NT, DH], F32, tag=tag, name="c_ps")
            for n in range(NT):
                nc.tensor.matmul(c_ps[:, n, :], lhsT=cst[:, n, :], rhs=dc[:, kind, :], start=True, stop=False)
                nc.tensor.matmul(c_ps[:, n, :], lhsT=cst[:, NT + n, :], rhs=ds[:, kind, :], start=False, stop=True)
            return c_ps

        def key_shift(pg):
            c_ps = shift_table(pg, 1, "kv")
            ck = work.tile([P, NT, DH], F32, tag="ck", name="ck")
            nc.scalar.copy(out=ck[:], in_=c_ps[:])
            ck_tiles[pg] = ck

        def query_shift(pg):
            cq_tiles[pg] = shift_table(pg, 0, "c")

        def front(gi, share=()):
            state[gi] = {"grouped": transpose_group(x_sb[gi], share, psum_t, "xt")}

        def quant(gi):
            st = state[gi]
            st["codes"] = deep.tile([P, NT * P], U32, tag="codes", name="codes", align_bytes=64)
            st["scales"] = deep.tile([P, NT * P], U8, tag="scales", name="scales", align_bytes=64)
            quantise(st["grouped"], st["codes"], st["scales"])

        def project(gi, row, bank):
            st = state[gi]
            for n in range(NT):
                nc.tensor.matmul_mx(
                    out=bank[:, n, :],
                    lhsT=st["codes"][:, n * P:(n + 1) * P].bitcast(FP8X4),
                    lhsT_scale=st["scales"][:, n * P:(n + 1) * P],
                    rhs=w_codes[:, row * P:(row + 1) * P].bitcast(FP8X4),
                    rhs_scale=w_scales[:, row * P:(row + 1) * P],
                    start=True,
                    stop=True,
                )

        def squares(gi, h, bank):
            st = state[gi]
            if "ss" not in st:
                st["ss"] = deep.tile([P, NH * NT], F32, tag="ss", name="ss")
            for n in range(NT):
                junk = work.tile([P, DH], BF16, tag="junk", name="junk")
                nc.scalar.activation(
                    out=junk[:], in_=bank[:, n, :], func=ACT.Square,
                    accum_out=st["ss"][:, h * NT + n:h * NT + n + 1],
                )

        def project_key(gi):
            bank = psum_s.tile([P, NT, DH], F32, tag="kv", name="kbank")
            project(gi, KEY, bank)
            squares(gi, KEY, bank)

        def project_key_t(gi):
            st = state[gi]
            st["kT"] = psum_s.tile([P, GROUP], F32, tag="kT", name="kT")
            for twice in range(2):
                nc.tensor.matmul_mx(
                    out=st["kT"][:],
                    lhsT=w_codes[:, KEY * P:(KEY + 1) * P].bitcast(FP8X4),
                    lhsT_scale=w_scales[:, KEY * P:(KEY + 1) * P],
                    rhs=st["codes"][:].bitcast(FP8X4),
                    rhs_scale=st["scales"][:],
                    start=True,
                    stop=True,
                )

        def project_value(gi):
            pg, b = order[gi]
            bank = psum_s.tile([P, NT, DH], F32, tag="kv", name="vbank")
            project(gi, VAL, bank)
            ov = deep.tile([P, NT, DH], F32, tag="ov", name="ov")
            nc.scalar.copy(out=ov[:], in_=bank[:])
            lo = pg * GROUP
            nc.sync.dma_start(
                out=out_2[b, 0, lo:lo + GROUP, :].rearrange("(p n) j -> p (n j)", n=NT),
                in_=ov[:].rearrange("p n j -> p (n j)"),
            )

        def project_query(gi, h):
            st = state[gi]
            bank = psum_q.tile([P, NT, DH], F32, tag="q", name="qbank")
            st["q%d" % h] = bank
            project(gi, h, bank)
            squares(gi, h, bank)

        def norm_root(gi):
            st = state[gi]
            st["rinv"] = deep.tile([P, NH * NT], F32, tag="rinv", name="rinv")
            nc.scalar.activation(
                out=st["rinv"][:], in_=st["ss"][:], func=ACT.Abs_reciprocal_sqrt, scale=1.0 / DH, bias=eps_t[:]
            )

        def products_key(gi):
            pg, b = order[gi]
            st = state[gi]
            st["pk"] = work.tile([P, 2, GROUP], F32, tag="pk", name="pk")
            nc.vector.tensor_tensor(
                out=st["pk"][:], in0=st["kT"][:].unsqueeze(1).to_broadcast([P, 2, GROUP]),
                in1=ktab[pg][:].rearrange("p (a n) r -> p a (n r)", a=2), op=ALU.mult,
            )

        def products_query(gi, h):
            pg, b = order[gi]
            st = state[gi]
            if h == 0:
                st["t12"] = prods.tile([P, 2, NQ, NT, 2, HALF], F32, tag="t12", name="t12")
            nc.vector.tensor_tensor(
                out=st["t12"][:, :, h, :, :, :].rearrange("p a n c j -> p a (n c j)"),
                in0=st["q%d" % h][:].rearrange("p n j -> p (n j)").unsqueeze(1).to_broadcast([P, 2, NT * DH]),
                in1=qtab[pg][:].rearrange("p a n j -> p a (n j)"),
                op=ALU.mult,
            )

        def join_key(gi):
            st = state[gi]
            tk = psum_s.tile([P, NT, DH], F32, tag="tk", name="tk")
            for n in range(NT):
                for a, moving in ((0, ident_f), (1, perm_f)):
                    nc.tensor.matmul(
                        tk[:, n, :], lhsT=st["pk"][:, a, n * P:(n + 1) * P], rhs=moving[:],
                        start=a == 0, stop=a == 1, is_transpose=True,
                    )
            st["tk"] = tk

        def scale_key(gi):
            st = state[gi]
            ks = work.tile([P, NT, DH], F32, tag="ks", name="ks")
            for n in range(NT):
                i = KEY * NT + n
                nc.scalar.activation(out=ks[:, n, :], in_=st["tk"][:, n, :], func=ACT.Copy, scale=st["rinv"][:, i:i + 1])
            st["ks"] = ks

        def finish_key(gi):
            pg, b = order[gi]
            st = state[gi]
            ok = deep.tile([P, NT, DH], F32, tag="ok", name="ok")
            nc.gpsimd.tensor_tensor(out=ok[:], in0=st["ks"][:], in1=ck_tiles[pg][:], op=ALU.add)
            store_key(gi, ok)

        def store_key(gi, ok):
            pg, b = order[gi]
            lo = pg * GROUP
            nc.sync.dma_start(
                out=out_1[b, 0, lo:lo + GROUP, :].rearrange("(p n) j -> p (n j)", n=NT),
                in_=ok[:].rearrange("p n j -> p (n j)"),
            )

        def join_query(eng, gi, h0, h1, dst):
            t12 = state[gi]["t12"]
            eng.tensor_tensor(
                out=dst.rearrange("p h n c j -> p (h n) c j"),
                in0=t12[:, 0, h0:h1, :, :, :].rearrange("p h n c j -> p (h n) c j"),
                in1=t12[:, 1, h0:h1, :, :, :].rearrange("p h n c j -> p (h n) c j")[:, :, ::-1, :],
                op=ALU.add,
            )

        def join_pool(gi):
            t3 = single.tile([P, NQ, NT, 2, HALF], F32, tag="t3", name="t3")
            join_query(nc.gpsimd, gi, 0, NQ, t3[:])
            state[gi]["sums"] = t3

        def join_last():
            t12 = state[NG - 1]["t12"]
            join_query(nc.gpsimd, NG - 1, 0, NQ, t12[:, 0, :, :, :, :])
            state[NG - 1]["sums"] = t12[:, 0, :, :, :, :]

        def finish_key_vector(gi):
            pg, b = order[gi]
            st = state[gi]
            ok = deep.tile([P, NT, DH], F32, tag="ok", name="ok")
            for n in range(NT):
                nc.vector.scalar_tensor_tensor(
                    out=ok[:, n, :], in0=st["tk"][:, n, :], scalar=st["rinv"][:, KEY * NT + n:KEY * NT + n + 1],
                    in1=ck_tiles[pg][:, n, :], op0=ALU.mult, op1=ALU.add,
                )
            store_key(gi, ok)

        def finish(gi, blocks):
            pg, b = order[gi]
            st = state[gi]
            if "oq" not in st:
                st["oq"] = deep.tile([P, NQ, NT, DH], F32, tag="oq", name="oq")
            for h, n in blocks:
                i = h * NT + n
                nc.vector.scalar_tensor_tensor(
                    out=st["oq"][:, h, n, :],
                    in0=st["sums"][:, h, n, :, :].rearrange("p c j -> p (c j)"),
                    scalar=st["rinv"][:, i:i + 1],
                    in1=cq_tiles[pg][:, n, :],
                    op0=ALU.mult,
                    op1=ALU.add,
                )

        def store(gi, h0, h1):
            pg, b = order[gi]
            lo = pg * GROUP
            nc.sync.dma_start(
                out=out_0[b, h0:h1, lo:lo + GROUP, :].rearrange("h (p n) j -> p h (n j)", n=NT),
                in_=state[gi]["oq"][:, h0:h1, :, :].rearrange("p h n j -> p h (n j)"),
            )

        all_blocks = [(h, n) for h in range(NQ) for n in range(NT)]
        banks = transpose_words(w_sb, psum_q, "q")
        w_grouped = new_grouped()
        interleave(w_grouped, banks, 0, False)
        interleave(w_grouped, banks, 1, True)
        quantise(w_grouped, w_codes, w_scales)
        spread_gains()
        shift_matrices()
        front(0, (1,))
        key_gain_columns()
        swap_sin(0)
        quant(0)
        query_table(nc.vector, 0, 0, 2)
        front(1)
        project_query(0, 0)
        quant(1)
        for pg in range(1, PG):
            swap_sin(pg)
        project_query(0, 1)
        transpose_table(0, psum_s, "c")
        banks = transpose_words(x_sb[2], psum_t, "xt")
        state[2] = {"grouped": new_grouped()}
        interleave(state[2]["grouped"], banks, 0, False)
        key_table(0)
        project_key(0)
        project_key_t(0)
        products_query(0, 0)
        project_query(1, 0)
        project_value(0)
        norm_root(0)
        products_query(0, 1)
        interleave(state[2]["grouped"], banks, 1, True)
        project_key(1)
        project_query(1, 1)
        front(3)
        project_value(1)
        norm_root(1)
        products_key(0)
        project_key_t(1)
        join_key(0)
        scale_key(0)
        query_shift(0)
        key_shift(0)
        for it in range(1, NG):
            last = it == NG - 1
            pg, step = divmod(it, B)
            join_pool(it - 1)
            if it > 1 and not last:
                finish_key(it - 1)
            if step == 1 and pg > 0:
                query_shift(pg)
            products_query(it, 0)
            if it == 1:
                quant(2)
                for a in range(2):
                    query_table(nc.gpsimd, 1, a, a + 1)
                finish_key(0)
            if not last:
                project_query(it + 1, 0)
                project_key(it + 1)
            products_query(it, 1)
            if not last:
                project_query(it + 1, 1)
            else:
                join_last()
            if it + 3 < NG:
                front(it + 3)
            if not last:
                project_value(it + 1)
                norm_root(it + 1)
            products_key(it)
            if not last:
                project_key_t(it + 1)
            join_key(it)
            if not last:
                scale_key(it)
            if step == 2 and pg + 1 < PG:
                key_shift(pg + 1)
            if it in (1, 4, 8):
                transpose_table((it + 4) // B, psum_s, "kv")
            finish(it - 1, all_blocks[:-1])
            if step == 3 and pg + 1 < PG:
                key_table(pg + 1)
            if it in (2, 5):
                query_table(nc.vector, it // 2 + 1, 0, 2)
            if it + 2 < NG:
                quant(it + 2)
            finish(it - 1, all_blocks[-1:])
            store(it - 1, 0, NQ)
        finish_key_vector(NG - 1)
        finish_key(NG - 2)
        for h in range(NQ):
            finish(NG - 1, all_blocks[h * NT:(h + 1) * NT])
            store(NG - 1, h, h + 1)
